import numpy as np
import ml_dtypes


def mxq(x, axis, fmt="e4m3"):
    dtype, down = {"e4m3": (ml_dtypes.float8_e4m3fn, 7), "e5m2": (ml_dtypes.float8_e5m2, 14)}[fmt]
    v = np.moveaxis(np.asarray(x, np.float32).astype(ml_dtypes.bfloat16).astype(np.float64), axis, -1)
    blocks = v.reshape(v.shape[:-1] + (-1, 32))
    amax = np.abs(blocks).max(-1, keepdims=True)
    byte = np.maximum(np.where(amax > 0, np.frexp(amax)[1] - 1 + 127, 0) - down, 1)
    scale = np.exp2(byte - 127.0)
    codes = (blocks / scale).astype(np.float32).astype(dtype).astype(np.float64)
    return np.moveaxis((codes * scale).reshape(v.shape), -1, axis)


WIDE = False


def mx_kscale(k):
    if not WIDE:
        return np.ones(k)
    levels = np.array([10, -10, 5, -5, 0])
    if k % 512:
        return np.exp2(np.random.permutation(np.resize(levels, k // 32))).repeat(32)
    a = np.empty((k // 512, 16))
    for p in range(k // 512):
        a[p, :8] = np.random.permutation(np.resize(levels, 8))
        for g in range(8):
            far = levels[np.abs(levels - a[p, g]) >= 10]
            a[p, g + 8] = far[np.random.randint(len(far))]
    return np.exp2(a.ravel()).repeat(32)


BF16 = ml_dtypes.bfloat16


def bf(x):
    return np.asarray(x, np.float32).astype(BF16)


def f64(x):
    return np.asarray(x).astype(np.float64)


B, M, D, E = 2, 512, 1024, 1024
HALF = E // 2


def rope_cos_sin():
    i = np.arange(HALF, dtype=np.float64)
    theta = np.power(10000.0, -2.0 * (i - 1.0) / E)
    pos = np.arange(M, dtype=np.float64)
    ang = pos[:, None] * theta[None, :]
    return np.cos(ang), np.sin(ang)


def rotate(t, cos, sin):
    te = t[..., 0::2]
    to = t[..., 1::2]
    re = te * cos + to * sin
    ro = -te * sin + to * cos
    return np.stack((re, ro), axis=-1).reshape(t.shape)


def draw0():
    s = mx_kscale(D)
    sc = 1.0 / np.sqrt(D)
    return {"x": bf(np.random.standard_normal((B, M, D)) * s),
            "w_q": bf(np.random.standard_normal((E, D)) * sc / s[None, :]),
            "w_k": bf(np.random.standard_normal((E, D)) * sc / s[None, :])}


def core(x, w_q, w_k):
    xq = mxq(f64(x), 2, "e4m3")
    q = xq @ mxq(f64(w_q).T, 0, "e4m3")
    k = xq @ mxq(f64(w_k).T, 0, "e4m3")
    cos, sin = rope_cos_sin()
    return rotate(q, cos, sin), rotate(k, cos, sin)


def e4m3fn_bytes(y):
    return np.clip(np.asarray(y, np.float64), -448.0, 448.0).astype(np.float32).astype(ml_dtypes.float8_e4m3fn).view(np.uint8)


def e4m3fn_values(b):
    return np.asarray(b, np.uint8).view(ml_dtypes.float8_e4m3fn).astype(np.float64)


def setup_inputs():
    d = draw0()
    x0 = np.asarray(d['x']).astype(np.float64)
    s = (np.max(np.abs(x0), axis=(0, 1), keepdims=True) / 448.0).astype(np.float32)
    out = {}
    for k, v in d.items():
        if k == 'x':
            out['x_bytes'] = e4m3fn_bytes(x0 / s.astype(np.float64))
            out['x_scale'] = s
        else:
            out[k] = v
    return out


def reference(x_bytes, x_scale, w_q, w_k):
    return core(e4m3fn_values(x_bytes) * x_scale.astype(np.float64), w_q, w_k)

@@ -1,0 +1,291 @@
+from contextlib import ExitStack
+
+import concourse.mybir as mybir
+from concourse.masks import make_identity
+
+B, M, D, E = 2, 512, 1024, 1024
+FLOPS = 2 * B * M * D * 2 * E
+
+F32 = mybir.dt.float32
+BF16 = mybir.dt.bfloat16
+U32 = mybir.dt.uint32
+I32 = mybir.dt.int32
+U8 = mybir.dt.uint8
+FP8 = mybir.dt.float8_e4m3fn
+FP8X4 = mybir.dt.float8_e4m3fn_x4
+ALU = mybir.AluOpType
+ACT = mybir.ActivationFunctionType
+
+P = 128
+HALF = E // 2
+PI = 3.141592653589793
+RATIO = 10000.0 ** (-1.0 / 512.0)
+
+
+def wrap_width(j):
+    last = P * (j + 1) - 1
+    i = 0
+    while last * RATIO ** (i - 1) >= PI:
+        i += 1
+    return 32 * ((i + 31) // 32)
+
+
+def tile_ropemaskedattentionhead_pa_kernel(tc, x_bytes, x_scale, w_q, w_k, out_0, out_1):
+    nc = tc.nc
+    outs = (out_0.flatten_outer_dims(), out_1.flatten_outer_dims())
+    weights = (w_q, w_k)
+
+    with ExitStack() as ctx:
+        const = ctx.enter_context(tc.tile_pool(name="const", bufs=1))
+        xwp = ctx.enter_context(tc.tile_pool(name="xwp", bufs=4))
+        xgp = ctx.enter_context(tc.tile_pool(name="xgp", bufs=4))
+        wgp = ctx.enter_context(tc.tile_pool(name="wgp", bufs=8))
+        chain = ctx.enter_context(tc.tile_pool(name="chain", bufs=2))
+        prp = ctx.enter_context(tc.tile_pool(name="prp", bufs=3))
+        otp = ctx.enter_context(tc.tile_pool(name="otp", bufs=3))
+        pst = ctx.enter_context(tc.psum_pool(name="pst", bufs=3))
+        psa = ctx.enter_context(tc.psum_pool(name="psa", bufs=4))
+        psw = ctx.enter_context(tc.psum_pool(name="psw", bufs=1))
+        ctx.enter_context(tc.manual_schedule(engines={mybir.EngineType.DVE, mybir.EngineType.Activation, mybir.EngineType.PE}))
+
+        sc = const.tile([P, D], F32, name="sc")
+        nc.scalar.dma_start(out=sc[:], in_=x_scale.rearrange("a b k -> (a b k)").partition_broadcast(P))
+        xview = x_bytes.rearrange("b s k -> (b s) k").rearrange("(a t p) k -> a p t k", t=2, p=P)
+        wviews = [w.rearrange("(cc a p) k -> cc p a k", a=2, p=P) for w in weights]
+        xb = []
+        wr = {}
+        for a in range(4):
+            t = const.tile([P, 2, D], U8, name="xb%d" % a)
+            nc.sync.dma_start(out=t[:], in_=xview[a])
+            xb.append(t)
+            t = const.tile([P, 2, D], BF16, name="wr0%d" % a)
+            nc.sync.dma_start(out=t[:], in_=wviews[0][a])
+            wr[(0, a)] = t
+        for cc in range(4):
+            t = const.tile([P, 2, D], BF16, name="wr1%d" % cc)
+            nc.sync.dma_start(out=t[:], in_=wviews[1][cc])
+            wr[(1, cc)] = t
+
+        pcol = const.tile([P, 4], F32, name="pcol")
+        nc.gpsimd.iota(pcol[:], pattern=[[P, 4]], base=0, channel_multiplier=1, allow_small_or_imprecise_dtypes=True)
+        ident = const.tile([P, P], F32, name="ident")
+        make_identity(nc, ident[:])
+        ones = const.tile([P, 1], F32, name="ones")
+        nc.vector.memset(ones[:], 1.0)
+        warm = const.tile([P, 1], F32, name="warm")
+        nc.scalar.activation(out=warm[:], in_=ones[:], func=ACT.Sin)
+        phi = const.tile([P, HALF], F32, name="phi")
+        nc.vector.tensor_scalar(out=phi[:, 0:1], in0=ones[:], scalar1=1.0 / (RATIO * 2.0 * PI), scalar2=None, op0=ALU.mult)
+        for s in range(9):
+            w = 2 ** s
+            nc.vector.tensor_scalar(out=phi[:, w : 2 * w], in0=phi[:, 0:w], scalar1=RATIO ** w, scalar2=None, op0=ALU.mult)
+        posp = const.tile([P, 4], F32, name="posp")
+        nc.vector.tensor_scalar(out=posp[:], in0=pcol[:], scalar1=2.0 * PI, scalar2=None, op0=ALU.mult)
+        negp = const.tile([P, 4], F32, name="negp")
+        nc.vector.tensor_scalar(out=negp[:], in0=pcol[:], scalar1=-2.0 * PI, scalar2=None, op0=ALU.mult)
+
+        xc = []
+        xs = []
+        for a in range(4):
+            xc.append(const.tile([P, 4 * P], U32, name="xc%d" % a, align_bytes=64))
+            xs.append(const.tile([P, 4 * P], U8, name="xs%d" % a, align_bytes=64))
+        wc = []
+        ws = []
+        for mat in range(2):
+            wc.append([const.tile([P, E], U32, name="wc%d%d" % (mat, g), align_bytes=64) for g in range(2)])
+            ws.append([const.tile([P, E], U8, name="ws%d%d" % (mat, g), align_bytes=64) for g in range(2)])
+        fracs = []
+        tab = []
+
+        def make_frac(j):
+            n = wrap_width(j)
+            turns = chain.tile([P, HALF], I32, name="turns")
+            nc.vector.tensor_scalar(out=turns[:, 0:n], in0=phi[:, 0:n], scalar1=pcol[:, j : j + 1], scalar2=None, op0=ALU.mult)
+            frac = const.tile([P, HALF], F32, name="frac%d" % j)
+            nc.vector.scalar_tensor_tensor(
+                out=frac[:, 0:n], in0=phi[:, 0:n], scalar=pcol[:, j : j + 1], in1=turns[:, 0:n], op0=ALU.mult, op1=ALU.subtract
+            )
+            fracs.append(frac)
+
+        def table_calls(j):
+            n = wrap_width(j)
+            rest = HALF - n
+            frac = fracs[j]
+            afrac = chain.tile([P, HALF], F32, name="afrac")
+            t = const.tile([P, 4, HALF], F32, name="tab%d" % j)
+            tab.append(t)
+            neg = negp[:, j : j + 1]
+            pos = posp[:, j : j + 1]
+            act = nc.scalar.activation
+            return [
+                lambda: act(out=afrac[:, 0:n], in_=frac[:, 0:n], func=ACT.Abs),
+                lambda: act(
+                    out=t[:, 0:2, 0:n],
+                    in_=afrac[:, 0:n].unsqueeze(1).to_broadcast([P, 2, n]),
+                    func=ACT.Sin,
+                    scale=-2.0 * PI,
+                    bias=0.5 * PI,
+                ),
+                lambda: act(out=t[:, 2, 0:n], in_=frac[:, 0:n], func=ACT.Sin, scale=-2.0 * PI),
+                lambda: act(out=t[:, 3, 0:n], in_=frac[:, 0:n], func=ACT.Sin, scale=2.0 * PI),
+                lambda: act(
+                    out=t[:, 0:2, n:HALF],
+                    in_=phi[:, n:HALF].unsqueeze(1).to_broadcast([P, 2, rest]),
+                    func=ACT.Sin,
+                    scale=neg,
+                    bias=0.5 * PI,
+                ),
+                lambda: act(out=t[:, 2, n:HALF], in_=phi[:, n:HALF], func=ACT.Sin, scale=neg),
+                lambda: act(out=t[:, 3, n:HALF], in_=phi[:, n:HALF], func=ACT.Sin, scale=pos),
+            ]
+
+        idle_bank = psw.tile([P, 512], F32, name="idle_bank")
+
+        def keep_warm():
+            for rep in range(1):
+                nc.tensor.matmul(out=idle_bank[:], lhsT=wr[(0, 0)][:, 0, 0:P], rhs=wr[(0, 0)][:, 0, 0:512], start=True, stop=True)
+
+        def widen(m):
+            xw = xwp.tile([P, D], BF16, name="xw")
+            nc.vector.tensor_tensor(out=xw[:], in0=xb[m // 2][:, m % 2, :].bitcast(FP8), in1=sc[:], op=ALU.mult)
+            return xw
+
+        def turn_x(xw, xg, t):
+            words = xw[:].bitcast(F32)
+            keep_warm()
+            tp = pst.tile([P, 2, 2, P], F32, name="tp")
+            for g in range(2):
+                for u in range(2):
+                    nc.tensor.transpose(tp[:, g, u, :], words[:, 256 * g + u : 256 * (g + 1) : 2], ident[:])
+            nc.scalar.copy(out=xg[:, t].bitcast(F32), in_=tp[:].rearrange("p g u r -> p g r u"))
+
+        def quant_x(a, xg):
+            nc.vector.quantize_mx(
+                out=xc[a][:].bitcast(FP8X4), scales=xs[a][:], in_=xg[:].rearrange("p t g r k -> p (t g r k)")
+            )
+
+        def turn_w(mat, cc, g, wg):
+            words = wr[(mat, cc)][:].bitcast(F32)
+            if mat == 0:
+                keep_warm()
+            tp = pst.tile([P, 2, 2, P], F32, name="tp")
+            for a in range(2):
+                for u in range(2):
+                    nc.tensor.transpose(tp[:, a, u, :], words[:, a, 256 * g + u : 256 * (g + 1) : 2], ident[:])
+            nc.scalar.copy(out=wg[:, cc % 2].bitcast(F32), in_=tp[:].rearrange("p a u r -> p a r u"))
+
+        def quant_w(mat, b, g, wg):
+            cols = slice(512 * b, 512 * (b + 1))
+            nc.vector.quantize_mx(
+                out=wc[mat][g][:, cols].bitcast(FP8X4),
+                scales=ws[mat][g][:, cols],
+                in_=wg[:].rearrange("p c a r k -> p (c a r k)"),
+            )
+
+        for j in range(2):
+            make_frac(j)
+        for call in table_calls(0):
+            call()
+        xgs = {}
+        wgs = {}
+        xws = {}
+        for m in range(4):
+            xws[m] = widen(m)
+        for a in range(4):
+            xg_new = xgp.tile([P, 2, 2, P, 4], BF16, name="xg", align_bytes=64)
+            xgs[a] = xg_new
+            if a % 2 == 0:
+                for g in range(2):
+                    wg_new = wgp.tile([P, 2, 2, P, 4], BF16, name="wg", align_bytes=64)
+                    wgs[(0, a // 2, g)] = wg_new
+            for g in range(2):
+                turn_w(0, a, g, wgs[(0, a // 2, g)])
+            for t in range(2):
+                turn_x(xws[2 * a + t], xg_new, t)
+            if a < 2:
+                xws[2 * a + 4] = widen(2 * a + 4)
+                xws[2 * a + 5] = widen(2 * a + 5)
+            if a == 1:
+                for j in range(2, 4):
+                    make_frac(j)
+            if a == 2:
+                quant_x(0, xgs[0])
+                quant_x(1, xgs[1])
+        for call in table_calls(1):
+            call()
+        quant_x(2, xgs[2])
+        quant_w(0, 0, 0, wgs[(0, 0, 0)])
+        quant_w(0, 0, 1, wgs[(0, 0, 1)])
+        quant_x(3, xgs[3])
+        quant_w(0, 1, 0, wgs[(0, 1, 0)])
+        quant_w(0, 1, 1, wgs[(0, 1, 1)])
+
+        def products(m, mat, between=None):
+            pr = prp.tile([P, 2, 2, 512], F32, name="pr")
+            tv = tab[m % 4][:].rearrange("p (rep e) i -> p rep i e", rep=2)
+            for b in range(2):
+                if b == 1 and between is not None:
+                    between()
+                acc = psa.tile([P, 512], F32, name="acc")
+                for g in range(2):
+                    xcols = slice((2 * (m % 2) + g) * P, (2 * (m % 2) + g + 1) * P)
+                    nc.tensor.matmul_mx(
+                        out=acc[:],
+                        lhsT=xc[m // 2][:, xcols].bitcast(FP8X4),
+                        lhsT_scale=xs[m // 2][:, xcols],
+                        rhs=wc[mat][g][:, 512 * b : 512 * (b + 1)].bitcast(FP8X4),
+                        rhs_scale=ws[mat][g][:, 512 * b : 512 * (b + 1)],
+                        start=(g == 0),
+                        stop=(g == 1),
+                    )
+                nc.vector.tensor_tensor(
+                    out=pr[:, :, b, :].rearrange("p rep (i e) -> p rep i e", e=2),
+                    in0=acc[:].rearrange("p (i e) -> p i e", e=2).unsqueeze(1).to_broadcast([P, 2, 256, 2]),
+                    in1=tv[:, :, 256 * b : 256 * (b + 1), :],
+                    op=ALU.mult,
+                )
+            return pr
+
+        def sums(m, mat, pr, on_vector):
+            ot = otp.tile([P, 2, 256, 2], F32, name="ot")
+            straight = pr[:, 0].rearrange("p b (i e) -> p b i e", e=2)
+            swapped = pr[:, 1].rearrange("p b (i e) -> p b i e", e=2)[:, :, :, ::-1]
+            rows = outs[mat][m * P : (m + 1) * P, :]
+            if on_vector:
+                for b in range(2):
+                    nc.vector.tensor_tensor(out=ot[:, b], in0=straight[:, b], in1=swapped[:, b], op=ALU.add)
+                    nc.sync.dma_start(out=rows[:, 512 * b : 512 * (b + 1)], in_=ot[:, b].rearrange("p i e -> p (i e)"))
+            else:
+                nc.gpsimd.tensor_tensor(out=ot[:], in0=straight, in1=swapped, op=ALU.add)
+                nc.sync.dma_start(out=rows, in_=ot[:].rearrange("p b i e -> p (b i e)"))
+
+        m_order = [m for j in range(4) for m in (j, j + 4)]
+        k_banks = [(b, g, c) for b in range(2) for g in range(2) for c in range(2)]
+        waiting = []
+        held = []
+
+        def middle_block():
+            for b in range(2):
+                for g in range(2):
+                    quant_w(1, b, g, wgs[(1, b, g)])
+            sums(m_order[6], 0, held[0], True)
+
+        for idx, m in enumerate(m_order):
+            if idx == 0 or idx == 2:
+                waiting.extend(table_calls(idx // 2 + 2))
+            pr = products(m, 0, middle_block if idx == 7 else None)
+            for b, g, c in k_banks[2 * idx : 2 * idx + 2]:
+                if c == 0:
+                    wg_new = wgp.tile([P, 2, 2, P, 4], BF16, name="wg", align_bytes=64)
+                    wgs[(1, b, g)] = wg_new
+                turn_w(1, 2 * b + c, g, wgs[(1, b, g)])
+            for call in waiting[0:4]:
+                call()
+            waiting = waiting[4:]
+            if idx == 6:
+                held.append(pr)
+            else:
+                sums(m, 0, pr, False)
+        for idx, m in enumerate(m_order):
+            pr = products(m, 1)
+            sums(m, 1, pr, idx == 7)

@@ -49,7 +49,8 @@ def tile_ropemaskedattentionhead_pa_kernel(tc, x_bytes, x_scale, w_q, w_k, out_0
         ctx.enter_context(tc.manual_schedule(engines={mybir.EngineType.DVE, mybir.EngineType.Activation, mybir.EngineType.PE}))
 
         sc = const.tile([P, D], F32, name="sc")
-        nc.scalar.dma_start(out=sc[:], in_=x_scale.rearrange("a b k -> (a b k)").partition_broadcast(P))
+        s8 = const.tile([P, 8], F32, name="s8")
+        nc.sync.dma_start(out=s8[:], in_=x_scale.rearrange("a b (p c) -> (a b p) c", c=8))
         xview = x_bytes.rearrange("b s k -> (b s) k").rearrange("(a t p) k -> a p t k", t=2, p=P)
         wviews = [w.rearrange("(cc a p) k -> cc p a k", a=2, p=P) for w in weights]
         xb = []
@@ -83,6 +84,15 @@ def tile_ropemaskedattentionhead_pa_kernel(tc, x_bytes, x_scale, w_q, w_k, out_0
         nc.vector.tensor_scalar(out=posp[:], in0=pcol[:], scalar1=2.0 * PI, scalar2=None, op0=ALU.mult)
         negp = const.tile([P, 4], F32, name="negp")
         nc.vector.tensor_scalar(out=negp[:], in0=pcol[:], scalar1=-2.0 * PI, scalar2=None, op0=ALU.mult)
+
+        def spread_scales():
+            for h in range(2):
+                bank = pst.tile([P, 2, 2, P], F32, name="tp")
+                for c in range(4):
+                    nc.tensor.transpose(bank[:, c // 2, c % 2, :], s8[:, 4 * h + c : 4 * h + c + 1].to_broadcast([P, P]), ident[:])
+                nc.scalar.copy(
+                    out=sc[:].rearrange("p (j c) -> p j c", c=8)[:, :, 4 * h : 4 * h + 4], in_=bank[:].rearrange("p a b j -> p j (a b)")
+                )
 
         xc = []
         xs = []
@@ -184,8 +194,12 @@ def tile_ropemaskedattentionhead_pa_kernel(tc, x_bytes, x_scale, w_q, w_k, out_0
 
         for j in range(2):
             make_frac(j)
-        for call in table_calls(0):
+        first_table = table_calls(0)
+        for call in first_table[4:7] + first_table[0:4]:
             call()
+        spread_scales()
+        for j in range(2, 4):
+            make_frac(j)
         xgs = {}
         wgs = {}
         xws = {}
@@ -205,9 +219,6 @@ def tile_ropemaskedattentionhead_pa_kernel(tc, x_bytes, x_scale, w_q, w_k, out_0
             if a < 2:
                 xws[2 * a + 4] = widen(2 * a + 4)
                 xws[2 * a + 5] = widen(2 * a + 5)
-            if a == 1:
-                for j in range(2, 4):
-                    make_frac(j)
             if a == 2:
                 quant_x(0, xgs[0])
                 quant_x(1, xgs[1])

@@ -49,8 +49,8 @@ def tile_ropemaskedattentionhead_pa_kernel(tc, x_bytes, x_scale, w_q, w_k, out_0
         ctx.enter_context(tc.manual_schedule(engines={mybir.EngineType.DVE, mybir.EngineType.Activation, mybir.EngineType.PE}))
 
         sc = const.tile([P, D], F32, name="sc")
-        s8 = const.tile([P, 8], F32, name="s8")
-        nc.sync.dma_start(out=s8[:], in_=x_scale.rearrange("a b (p c) -> (a b p) c", c=8))
+        s8 = const.tile([P, 2, 4], F32, name="s8")
+        nc.sync.dma_start(out=s8[:], in_=x_scale.rearrange("a b (h p c) -> (a b p) h c", h=2, c=4))
         xview = x_bytes.rearrange("b s k -> (b s) k").rearrange("(a t p) k -> a p t k", t=2, p=P)
         wviews = [w.rearrange("(cc a p) k -> cc p a k", a=2, p=P) for w in weights]
         xb = []
@@ -71,6 +71,8 @@ def tile_ropemaskedattentionhead_pa_kernel(tc, x_bytes, x_scale, w_q, w_k, out_0
         nc.gpsimd.iota(pcol[:], pattern=[[P, 4]], base=0, channel_multiplier=1, allow_small_or_imprecise_dtypes=True)
         ident = const.tile([P, P], F32, name="ident")
         make_identity(nc, ident[:])
+        blank = const.tile([P, 512], BF16, name="blank")
+        nc.vector.memset(blank[:], 0.0)
         ones = const.tile([P, 1], F32, name="ones")
         nc.vector.memset(ones[:], 1.0)
         warm = const.tile([P, 1], F32, name="warm")
@@ -85,14 +87,13 @@ def tile_ropemaskedattentionhead_pa_kernel(tc, x_bytes, x_scale, w_q, w_k, out_0
         negp = const.tile([P, 4], F32, name="negp")
         nc.vector.tensor_scalar(out=negp[:], in0=pcol[:], scalar1=-2.0 * PI, scalar2=None, op0=ALU.mult)
 
-        def spread_scales():
-            for h in range(2):
-                bank = pst.tile([P, 2, 2, P], F32, name="tp")
-                for c in range(4):
-                    nc.tensor.transpose(bank[:, c // 2, c % 2, :], s8[:, 4 * h + c : 4 * h + c + 1].to_broadcast([P, P]), ident[:])
-                nc.scalar.copy(
-                    out=sc[:].rearrange("p (j c) -> p j c", c=8)[:, :, 4 * h : 4 * h + 4], in_=bank[:].rearrange("p a b j -> p j (a b)")
-                )
+        def spread_scales(h):
+            bank = pst.tile([P, 2, 2, P], F32, name="tp")
+            for c in range(4):
+                nc.tensor.transpose(bank[:, c // 2, c % 2, :], s8[:, h, c : c + 1].to_broadcast([P, P]), ident[:])
+            nc.scalar.copy(
+                out=sc[:, 512 * h : 512 * (h + 1)].rearrange("p (j c) -> p j c", c=4), in_=bank[:].rearrange("p a b j -> p j (a b)")
+            )
 
         xc = []
         xs = []
@@ -155,9 +156,12 @@ def tile_ropemaskedattentionhead_pa_kernel(tc, x_bytes, x_scale, w_q, w_k, out_0
             for rep in range(1):
                 nc.tensor.matmul(out=idle_bank[:], lhsT=wr[(0, 0)][:, 0, 0:P], rhs=wr[(0, 0)][:, 0, 0:512], start=True, stop=True)
 
+        def widen_part(m, xw, cols):
+            nc.vector.tensor_tensor(out=xw[:, cols], in0=xb[m // 2][:, m % 2, cols].bitcast(FP8), in1=sc[:, cols], op=ALU.mult)
+
         def widen(m):
             xw = xwp.tile([P, D], BF16, name="xw")
-            nc.vector.tensor_tensor(out=xw[:], in0=xb[m // 2][:, m % 2, :].bitcast(FP8), in1=sc[:], op=ALU.mult)
+            widen_part(m, xw, slice(0, D))
             return xw
 
         def turn_x(xw, xg, t):
@@ -195,16 +199,27 @@ def tile_ropemaskedattentionhead_pa_kernel(tc, x_bytes, x_scale, w_q, w_k, out_0
         for j in range(2):
             make_frac(j)
         first_table = table_calls(0)
-        for call in first_table[4:7] + first_table[0:4]:
+        for call in first_table[4:7]:
             call()
-        spread_scales()
+        for rep in range(5):
+            nc.tensor.matmul(out=idle_bank[:], lhsT=blank[:, 0:P], rhs=blank[:], start=True, stop=True)
+        for h in range(2):
+            spread_scales(h)
+        for call in first_table[0:4]:
+            call()
         for j in range(2, 4):
             make_frac(j)
         xgs = {}
         wgs = {}
         xws = {}
         for m in range(4):
-            xws[m] = widen(m)
+            xw_new = xwp.tile([P, D], BF16, name="xw")
+            xws[m] = xw_new
+        for h in range(2):
+            for m in range(2):
+                widen_part(m, xws[m], slice(512 * h, 512 * (h + 1)))
+        for m in range(2, 4):
+            widen_part(m, xws[m], slice(0, D))
         for a in range(4):
             xg_new = xgp.tile([P, 2, 2, P, 4], BF16, name="xg", align_bytes=64)
             xgs[a] = xg_new

@@ -67,14 +67,14 @@ def tile_ropemaskedattentionhead_pa_kernel(tc, x_bytes, x_scale, w_q, w_k, out_0
             nc.sync.dma_start(out=t[:], in_=wviews[1][cc])
             wr[(1, cc)] = t
 
+        ones = const.tile([P, 1], F32, name="ones")
+        nc.gpsimd.memset(ones[:], 1.0)
+        blank = const.tile([P, 512], BF16, name="blank")
+        nc.gpsimd.memset(blank[:], 0.0)
         pcol = const.tile([P, 4], F32, name="pcol")
         nc.gpsimd.iota(pcol[:], pattern=[[P, 4]], base=0, channel_multiplier=1, allow_small_or_imprecise_dtypes=True)
         ident = const.tile([P, P], F32, name="ident")
         make_identity(nc, ident[:])
-        blank = const.tile([P, 512], BF16, name="blank")
-        nc.vector.memset(blank[:], 0.0)
-        ones = const.tile([P, 1], F32, name="ones")
-        nc.vector.memset(ones[:], 1.0)
         warm = const.tile([P, 1], F32, name="warm")
         nc.scalar.activation(out=warm[:], in_=ones[:], func=ACT.Sin)
         phi = const.tile([P, HALF], F32, name="phi")
@@ -83,9 +83,9 @@ def tile_ropemaskedattentionhead_pa_kernel(tc, x_bytes, x_scale, w_q, w_k, out_0
             w = 2 ** s
             nc.vector.tensor_scalar(out=phi[:, w : 2 * w], in0=phi[:, 0:w], scalar1=RATIO ** w, scalar2=None, op0=ALU.mult)
         posp = const.tile([P, 4], F32, name="posp")
-        nc.vector.tensor_scalar(out=posp[:], in0=pcol[:], scalar1=2.0 * PI, scalar2=None, op0=ALU.mult)
+        nc.gpsimd.tensor_scalar(out=posp[:], in0=pcol[:], scalar1=2.0 * PI, scalar2=0.0, op0=ALU.mult, op1=ALU.add)
         negp = const.tile([P, 4], F32, name="negp")
-        nc.vector.tensor_scalar(out=negp[:], in0=pcol[:], scalar1=-2.0 * PI, scalar2=None, op0=ALU.mult)
+        nc.gpsimd.tensor_scalar(out=negp[:], in0=pcol[:], scalar1=-2.0 * PI, scalar2=0.0, op0=ALU.mult, op1=ALU.add)
 
         def spread_scales(h):
             bank = pst.tile([P, 2, 2, P], F32, name="tp")
@@ -242,9 +242,9 @@ def tile_ropemaskedattentionhead_pa_kernel(tc, x_bytes, x_scale, w_q, w_k, out_0
         quant_x(2, xgs[2])
         quant_w(0, 0, 0, wgs[(0, 0, 0)])
         quant_w(0, 0, 1, wgs[(0, 0, 1)])
-        quant_x(3, xgs[3])
         quant_w(0, 1, 0, wgs[(0, 1, 0)])
         quant_w(0, 1, 1, wgs[(0, 1, 1)])
+        quant_x(3, xgs[3])
 
         def products(m, mat, between=None):
             pr = prp.tile([P, 2, 2, 512], F32, name="pr")
@@ -272,7 +272,7 @@ def tile_ropemaskedattentionhead_pa_kernel(tc, x_bytes, x_scale, w_q, w_k, out_0
                 )
             return pr
 
-        def sums(m, mat, pr, on_vector):
+        def sums(m, mat, pr, on_vector, by_bank=False):
             ot = otp.tile([P, 2, 256, 2], F32, name="ot")
             straight = pr[:, 0].rearrange("p b (i e) -> p b i e", e=2)
             swapped = pr[:, 1].rearrange("p b (i e) -> p b i e", e=2)[:, :, :, ::-1]
@@ -281,6 +281,10 @@ def tile_ropemaskedattentionhead_pa_kernel(tc, x_bytes, x_scale, w_q, w_k, out_0
                 for b in range(2):
                     nc.vector.tensor_tensor(out=ot[:, b], in0=straight[:, b], in1=swapped[:, b], op=ALU.add)
                     nc.sync.dma_start(out=rows[:, 512 * b : 512 * (b + 1)], in_=ot[:, b].rearrange("p i e -> p (i e)"))
+            elif by_bank:
+                for b in range(2):
+                    nc.gpsimd.tensor_tensor(out=ot[:, b], in0=straight[:, b], in1=swapped[:, b], op=ALU.add)
+                nc.sync.dma_start(out=rows, in_=ot[:].rearrange("p b i e -> p (b i e)"))
             else:
                 nc.gpsimd.tensor_tensor(out=ot[:], in0=straight, in1=swapped, op=ALU.add)
                 nc.sync.dma_start(out=rows, in_=ot[:].rearrange("p b i e -> p (b i e)"))
@@ -288,13 +292,11 @@ def tile_ropemaskedattentionhead_pa_kernel(tc, x_bytes, x_scale, w_q, w_k, out_0
         m_order = [m for j in range(4) for m in (j, j + 4)]
         k_banks = [(b, g, c) for b in range(2) for g in range(2) for c in range(2)]
         waiting = []
-        held = []
 
         def middle_block():
             for b in range(2):
                 for g in range(2):
                     quant_w(1, b, g, wgs[(1, b, g)])
-            sums(m_order[6], 0, held[0], True)
 
         for idx, m in enumerate(m_order):
             if idx == 0 or idx == 2:
@@ -308,10 +310,7 @@ def tile_ropemaskedattentionhead_pa_kernel(tc, x_bytes, x_scale, w_q, w_k, out_0
             for call in waiting[0:4]:
                 call()
             waiting = waiting[4:]
-            if idx == 6:
-                held.append(pr)
-            else:
-                sums(m, 0, pr, False)
+            sums(m, 0, pr, False, by_bank=(idx in (0, 5, 6)))
         for idx, m in enumerate(m_order):
             pr = products(m, 1)
             sums(m, 1, pr, idx == 7)

@@ -67,14 +67,14 @@ def tile_ropemaskedattentionhead_pa_kernel(tc, x_bytes, x_scale, w_q, w_k, out_0
             nc.sync.dma_start(out=t[:], in_=wviews[1][cc])
             wr[(1, cc)] = t
 
-        ones = const.tile([P, 1], F32, name="ones")
-        nc.gpsimd.memset(ones[:], 1.0)
-        blank = const.tile([P, 512], BF16, name="blank")
-        nc.gpsimd.memset(blank[:], 0.0)
         pcol = const.tile([P, 4], F32, name="pcol")
         nc.gpsimd.iota(pcol[:], pattern=[[P, 4]], base=0, channel_multiplier=1, allow_small_or_imprecise_dtypes=True)
         ident = const.tile([P, P], F32, name="ident")
         make_identity(nc, ident[:])
+        blank = const.tile([P, 512], BF16, name="blank")
+        nc.vector.memset(blank[:], 0.0)
+        ones = const.tile([P, 1], F32, name="ones")
+        nc.vector.memset(ones[:], 1.0)
         warm = const.tile([P, 1], F32, name="warm")
         nc.scalar.activation(out=warm[:], in_=ones[:], func=ACT.Sin)
         phi = const.tile([P, HALF], F32, name="phi")
@@ -83,9 +83,9 @@ def tile_ropemaskedattentionhead_pa_kernel(tc, x_bytes, x_scale, w_q, w_k, out_0
             w = 2 ** s
             nc.vector.tensor_scalar(out=phi[:, w : 2 * w], in0=phi[:, 0:w], scalar1=RATIO ** w, scalar2=None, op0=ALU.mult)
         posp = const.tile([P, 4], F32, name="posp")
-        nc.gpsimd.tensor_scalar(out=posp[:], in0=pcol[:], scalar1=2.0 * PI, scalar2=0.0, op0=ALU.mult, op1=ALU.add)
+        nc.vector.tensor_scalar(out=posp[:], in0=pcol[:], scalar1=2.0 * PI, scalar2=None, op0=ALU.mult)
         negp = const.tile([P, 4], F32, name="negp")
-        nc.gpsimd.tensor_scalar(out=negp[:], in0=pcol[:], scalar1=-2.0 * PI, scalar2=0.0, op0=ALU.mult, op1=ALU.add)
+        nc.vector.tensor_scalar(out=negp[:], in0=pcol[:], scalar1=-2.0 * PI, scalar2=None, op0=ALU.mult)
 
         def spread_scales(h):
             bank = pst.tile([P, 2, 2, P], F32, name="tp")

@@ -39,7 +39,7 @@ def tile_ropemaskedattentionhead_pa_kernel(tc, x_bytes, x_scale, w_q, w_k, out_0
         const = ctx.enter_context(tc.tile_pool(name="const", bufs=1))
         xwp = ctx.enter_context(tc.tile_pool(name="xwp", bufs=4))
         xgp = ctx.enter_context(tc.tile_pool(name="xgp", bufs=4))
-        wgp = ctx.enter_context(tc.tile_pool(name="wgp", bufs=8))
+        wgp = ctx.enter_context(tc.tile_pool(name="wgp", bufs=4))
         chain = ctx.enter_context(tc.tile_pool(name="chain", bufs=2))
         prp = ctx.enter_context(tc.tile_pool(name="prp", bufs=3))
         otp = ctx.enter_context(tc.tile_pool(name="otp", bufs=3))
@@ -178,7 +178,7 @@ def tile_ropemaskedattentionhead_pa_kernel(tc, x_bytes, x_scale, w_q, w_k, out_0
                 out=xc[a][:].bitcast(FP8X4), scales=xs[a][:], in_=xg[:].rearrange("p t g r k -> p (t g r k)")
             )
 
-        def turn_w(mat, cc, g, wg):
+        def turn_w(mat, cc, g, wg, slot=None):
             words = wr[(mat, cc)][:].bitcast(F32)
             if mat == 0:
                 keep_warm()
@@ -186,7 +186,7 @@ def tile_ropemaskedattentionhead_pa_kernel(tc, x_bytes, x_scale, w_q, w_k, out_0
             for a in range(2):
                 for u in range(2):
                     nc.tensor.transpose(tp[:, a, u, :], words[:, a, 256 * g + u : 256 * (g + 1) : 2], ident[:])
-            nc.scalar.copy(out=wg[:, cc % 2].bitcast(F32), in_=tp[:].rearrange("p a u r -> p a r u"))
+            nc.scalar.copy(out=wg[:, cc % 2 if slot is None else slot].bitcast(F32), in_=tp[:].rearrange("p a u r -> p a r u"))
 
         def quant_w(mat, b, g, wg):
             cols = slice(512 * b, 512 * (b + 1))
@@ -293,24 +293,24 @@ def tile_ropemaskedattentionhead_pa_kernel(tc, x_bytes, x_scale, w_q, w_k, out_0
         k_banks = [(b, g, c) for b in range(2) for g in range(2) for c in range(2)]
         waiting = []
 
+        wide = [const.tile([P, 4, 2, P, 4], BF16, name="wide%d" % g, align_bytes=64) for g in range(2)]
+
         def middle_block():
-            for b in range(2):
-                for g in range(2):
-                    quant_w(1, b, g, wgs[(1, b, g)])
+            for g in range(2):
+                nc.vector.quantize_mx(
+                    out=wc[1][g][:].bitcast(FP8X4), scales=ws[1][g][:], in_=wide[g][:].rearrange("p c a r k -> p (c a r k)")
+                )
 
         for idx, m in enumerate(m_order):
             if idx == 0 or idx == 2:
                 waiting.extend(table_calls(idx // 2 + 2))
             pr = products(m, 0, middle_block if idx == 7 else None)
             for b, g, c in k_banks[2 * idx : 2 * idx + 2]:
-                if c == 0:
-                    wg_new = wgp.tile([P, 2, 2, P, 4], BF16, name="wg", align_bytes=64)
-                    wgs[(1, b, g)] = wg_new
-                turn_w(1, 2 * b + c, g, wgs[(1, b, g)])
+                turn_w(1, 2 * b + c, g, wide[g], slot=2 * b + c)
             for call in waiting[0:4]:
                 call()
             waiting = waiting[4:]
-            sums(m, 0, pr, False, by_bank=(idx in (0, 5, 6)))
+            sums(m, 0, pr, False, by_bank=(idx == 6))
         for idx, m in enumerate(m_order):
             pr = products(m, 1)
             sums(m, 1, pr, idx == 7)

@@ -311,6 +311,26 @@ def tile_ropemaskedattentionhead_pa_kernel(tc, x_bytes, x_scale, w_q, w_k, out_0
                 call()
             waiting = waiting[4:]
             sums(m, 0, pr, False, by_bank=(idx == 6))
+        shared = []
         for idx, m in enumerate(m_order):
             pr = products(m, 1)
-            sums(m, 1, pr, idx == 7)
+            if idx == 6:
+                ot6 = otp.tile([P, 2, 256, 2], F32, name="ot")
+                shared.extend([m, pr, ot6])
+                nc.gpsimd.tensor_tensor(
+                    out=ot6[:, 0],
+                    in0=pr[:, 0, 0].rearrange("p (i e) -> p i e", e=2),
+                    in1=pr[:, 1, 0].rearrange("p (i e) -> p i e", e=2)[:, :, ::-1],
+                    op=ALU.add,
+                )
+            else:
+                if idx == 7:
+                    m6, pr6, ot6 = shared
+                    nc.vector.tensor_tensor(
+                        out=ot6[:, 1],
+                        in0=pr6[:, 0, 1].rearrange("p (i e) -> p i e", e=2),
+                        in1=pr6[:, 1, 1].rearrange("p (i e) -> p i e", e=2)[:, :, ::-1],
+                        op=ALU.add,
+                    )
+                    nc.sync.dma_start(out=outs[1][m6 * P : (m6 + 1) * P, :], in_=ot6[:].rearrange("p b i e -> p (b i e)"))
+                sums(m, 1, pr, idx == 7)

@@ -18,8 +18,10 @@ ACT = mybir.ActivationFunctionType
 
 P = 128
 HALF = E // 2
+Q = 256
 PI = 3.141592653589793
 RATIO = 10000.0 ** (-1.0 / 512.0)
+ROOT2 = 2.0 ** 0.5
 
 
 def wrap_width(j):
@@ -32,49 +34,58 @@ def wrap_width(j):
 
 def tile_ropemaskedattentionhead_pa_kernel(tc, x_bytes, x_scale, w_q, w_k, out_0, out_1):
     nc = tc.nc
-    outs = (out_0.flatten_outer_dims(), out_1.flatten_outer_dims())
+    outs = [o.rearrange("b (j p) c -> j p b c", p=P) for o in (out_0, out_1)]
     weights = (w_q, w_k)
 
     with ExitStack() as ctx:
         const = ctx.enter_context(tc.tile_pool(name="const", bufs=1))
-        xwp = ctx.enter_context(tc.tile_pool(name="xwp", bufs=4))
-        xgp = ctx.enter_context(tc.tile_pool(name="xgp", bufs=4))
-        wgp = ctx.enter_context(tc.tile_pool(name="wgp", bufs=4))
+        xgp = ctx.enter_context(tc.tile_pool(name="xgp", bufs=3))
+        wgp = ctx.enter_context(tc.tile_pool(name="wgp", bufs=6))
         chain = ctx.enter_context(tc.tile_pool(name="chain", bufs=2))
         prp = ctx.enter_context(tc.tile_pool(name="prp", bufs=3))
-        otp = ctx.enter_context(tc.tile_pool(name="otp", bufs=3))
+        otp = ctx.enter_context(tc.tile_pool(name="otp", bufs=4))
         pst = ctx.enter_context(tc.psum_pool(name="pst", bufs=3))
-        psa = ctx.enter_context(tc.psum_pool(name="psa", bufs=4))
-        psw = ctx.enter_context(tc.psum_pool(name="psw", bufs=1))
-        ctx.enter_context(tc.manual_schedule(engines={mybir.EngineType.DVE, mybir.EngineType.Activation, mybir.EngineType.PE}))
+        psa = ctx.enter_context(tc.psum_pool(name="psa", bufs=3))
+        pss = ctx.enter_context(tc.psum_pool(name="pss", bufs=2))
+        ctx.enter_context(tc.manual_schedule(engines={mybir.EngineType.DVE, mybir.EngineType.Activation, mybir.EngineType.PE, mybir.EngineType.SP}))
 
-        sc = const.tile([P, D], F32, name="sc")
         s8 = const.tile([P, 2, 4], F32, name="s8")
         nc.sync.dma_start(out=s8[:], in_=x_scale.rearrange("a b (h p c) -> (a b p) h c", h=2, c=4))
-        xview = x_bytes.rearrange("b s k -> (b s) k").rearrange("(a t p) k -> a p t k", t=2, p=P)
-        wviews = [w.rearrange("(cc a p) k -> cc p a k", a=2, p=P) for w in weights]
-        xb = []
+        xview = x_bytes.rearrange("b (j p) k -> j p b k", p=P)
+        straight = [w.rearrange("(cc a p) k -> cc p a k", a=2, p=P) for w in weights]
+        paired = [w.rearrange("(cc p e) k -> cc p e k", e=2, p=P) for w in weights]
+        xb = {}
         wr = {}
-        for a in range(4):
-            t = const.tile([P, 2, D], U8, name="xb%d" % a)
-            nc.sync.dma_start(out=t[:], in_=xview[a])
-            xb.append(t)
-            t = const.tile([P, 2, D], BF16, name="wr0%d" % a)
-            nc.sync.dma_start(out=t[:], in_=wviews[0][a])
-            wr[(0, a)] = t
+
+        def load_x(j):
+            t = const.tile([P, 2, D], U8, name="xb%d" % j)
+            nc.sync.dma_start(out=t[:], in_=xview[j])
+            xb[j] = t
+
+        def load_w(mat, cc):
+            t = const.tile([P, 2, D], BF16, name="wr%d%d" % (mat, cc))
+            nc.sync.dma_start(out=t[:], in_=(straight if cc < 2 else paired)[mat][cc])
+            wr[(mat, cc)] = t
+
+        load_x(0)
+        load_w(0, 0)
+        load_w(0, 1)
+        load_x(1)
+        load_w(0, 2)
+        load_w(0, 3)
         for cc in range(4):
-            t = const.tile([P, 2, D], BF16, name="wr1%d" % cc)
-            nc.sync.dma_start(out=t[:], in_=wviews[1][cc])
-            wr[(1, cc)] = t
+            load_w(1, cc)
+        load_x(2)
+        load_x(3)
 
         pcol = const.tile([P, 4], F32, name="pcol")
         nc.gpsimd.iota(pcol[:], pattern=[[P, 4]], base=0, channel_multiplier=1, allow_small_or_imprecise_dtypes=True)
         ident = const.tile([P, P], F32, name="ident")
         make_identity(nc, ident[:])
-        blank = const.tile([P, 512], BF16, name="blank")
-        nc.vector.memset(blank[:], 0.0)
         ones = const.tile([P, 1], F32, name="ones")
         nc.vector.memset(ones[:], 1.0)
+        blank = const.tile([P, 512], BF16, name="blank")
+        nc.vector.memset(blank[:], 0.0)
         warm = const.tile([P, 1], F32, name="warm")
         nc.scalar.activation(out=warm[:], in_=ones[:], func=ACT.Sin)
         phi = const.tile([P, HALF], F32, name="phi")
@@ -87,26 +98,21 @@ def tile_ropemaskedattentionhead_pa_kernel(tc, x_bytes, x_scale, w_q, w_k, out_0
         negp = const.tile([P, 4], F32, name="negp")
         nc.vector.tensor_scalar(out=negp[:], in0=pcol[:], scalar1=-2.0 * PI, scalar2=None, op0=ALU.mult)
 
-        def spread_scales(h):
-            bank = pst.tile([P, 2, 2, P], F32, name="tp")
-            for c in range(4):
-                nc.tensor.transpose(bank[:, c // 2, c % 2, :], s8[:, h, c : c + 1].to_broadcast([P, P]), ident[:])
-            nc.scalar.copy(
-                out=sc[:, 512 * h : 512 * (h + 1)].rearrange("p (j c) -> p j c", c=4), in_=bank[:].rearrange("p a b j -> p j (a b)")
-            )
-
         xc = []
         xs = []
-        for a in range(4):
-            xc.append(const.tile([P, 4 * P], U32, name="xc%d" % a, align_bytes=64))
-            xs.append(const.tile([P, 4 * P], U8, name="xs%d" % a, align_bytes=64))
+        for j in range(4):
+            xc.append(const.tile([P, 4 * P], U32, name="xc%d" % j, align_bytes=64))
+            xs.append(const.tile([P, 4 * P], U8, name="xs%d" % j, align_bytes=64))
         wc = []
         ws = []
         for mat in range(2):
             wc.append([const.tile([P, E], U32, name="wc%d%d" % (mat, g), align_bytes=64) for g in range(2)])
             ws.append([const.tile([P, E], U8, name="ws%d%d" % (mat, g), align_bytes=64) for g in range(2)])
-        fracs = []
-        tab = []
+
+        fracs = {}
+        low = {}
+        high = {}
+        act = nc.scalar.activation
 
         def make_frac(j):
             n = wrap_width(j)
@@ -116,221 +122,294 @@ def tile_ropemaskedattentionhead_pa_kernel(tc, x_bytes, x_scale, w_q, w_k, out_0
             nc.vector.scalar_tensor_tensor(
                 out=frac[:, 0:n], in0=phi[:, 0:n], scalar=pcol[:, j : j + 1], in1=turns[:, 0:n], op0=ALU.mult, op1=ALU.subtract
             )
-            fracs.append(frac)
+            fracs[j] = frac
 
-        def table_calls(j):
-            n = wrap_width(j)
-            rest = HALF - n
+        def low_table(j):
+            n = min(Q, wrap_width(j))
             frac = fracs[j]
-            afrac = chain.tile([P, HALF], F32, name="afrac")
-            t = const.tile([P, 4, HALF], F32, name="tab%d" % j)
-            tab.append(t)
+            t = const.tile([P, 4, Q], F32, name="low%d" % j)
+            low[j] = t
             neg = negp[:, j : j + 1]
             pos = posp[:, j : j + 1]
-            act = nc.scalar.activation
-            return [
-                lambda: act(out=afrac[:, 0:n], in_=frac[:, 0:n], func=ACT.Abs),
-                lambda: act(
-                    out=t[:, 0:2, 0:n],
-                    in_=afrac[:, 0:n].unsqueeze(1).to_broadcast([P, 2, n]),
-                    func=ACT.Sin,
-                    scale=-2.0 * PI,
-                    bias=0.5 * PI,
-                ),
-                lambda: act(out=t[:, 2, 0:n], in_=frac[:, 0:n], func=ACT.Sin, scale=-2.0 * PI),
-                lambda: act(out=t[:, 3, 0:n], in_=frac[:, 0:n], func=ACT.Sin, scale=2.0 * PI),
-                lambda: act(
-                    out=t[:, 0:2, n:HALF],
-                    in_=phi[:, n:HALF].unsqueeze(1).to_broadcast([P, 2, rest]),
+            if n < Q:
+                act(
+                    out=t[:, 0:2, n:Q],
+                    in_=phi[:, n:Q].unsqueeze(1).to_broadcast([P, 2, Q - n]),
                     func=ACT.Sin,
                     scale=neg,
                     bias=0.5 * PI,
-                ),
-                lambda: act(out=t[:, 2, n:HALF], in_=phi[:, n:HALF], func=ACT.Sin, scale=neg),
-                lambda: act(out=t[:, 3, n:HALF], in_=phi[:, n:HALF], func=ACT.Sin, scale=pos),
-            ]
+                )
+                act(out=t[:, 2, n:Q], in_=phi[:, n:Q], func=ACT.Sin, scale=neg)
+                act(out=t[:, 3, n:Q], in_=phi[:, n:Q], func=ACT.Sin, scale=pos)
+            afrac = chain.tile([P, Q], F32, name="afrac")
+            act(out=afrac[:, 0:n], in_=frac[:, 0:n], func=ACT.Abs)
+            act(
+                out=t[:, 0:2, 0:n],
+                in_=afrac[:, 0:n].unsqueeze(1).to_broadcast([P, 2, n]),
+                func=ACT.Sin,
+                scale=-2.0 * PI,
+                bias=0.5 * PI,
+            )
+            act(out=t[:, 2, 0:n], in_=frac[:, 0:n], func=ACT.Sin, scale=-2.0 * PI)
+            act(out=t[:, 3, 0:n], in_=frac[:, 0:n], func=ACT.Sin, scale=2.0 * PI)
 
-        idle_bank = psw.tile([P, 512], F32, name="idle_bank")
+        def high_table(j):
+            n = max(Q, wrap_width(j)) - Q
+            t = const.tile([P, 3, Q], F32, name="high%d" % j)
+            high[j] = t
+            neg = negp[:, j : j + 1]
+            pos = posp[:, j : j + 1]
+            rest = phi[:, Q + n : HALF]
+            act(out=t[:, 0, n:Q], in_=rest, func=ACT.Sin, scale=neg, bias=0.5 * PI)
+            act(out=t[:, 1, n:Q], in_=rest, func=ACT.Sin, scale=pos, bias=-0.25 * PI)
+            act(out=t[:, 2, n:Q], in_=rest, func=ACT.Sin, scale=pos, bias=-0.75 * PI)
+            if n > 0:
+                frac = fracs[j][:, Q : Q + n]
+                afrac = chain.tile([P, 3, 32], F32, name="afrac3")
+                for r, shift in enumerate((0.0, 0.125, -0.125)):
+                    act(out=afrac[:, r, 0:n], in_=frac, func=ACT.Abs, bias=shift)
+                act(out=t[:, 0, 0:n], in_=afrac[:, 0, 0:n], func=ACT.Sin, scale=-2.0 * PI, bias=0.5 * PI)
+                act(out=t[:, 1:3, 0:n], in_=afrac[:, 1:3, 0:n], func=ACT.Sin, scale=2.0 * PI, bias=-0.5 * PI)
 
-        def keep_warm():
-            for rep in range(1):
-                nc.tensor.matmul(out=idle_bank[:], lhsT=wr[(0, 0)][:, 0, 0:P], rhs=wr[(0, 0)][:, 0, 0:512], start=True, stop=True)
+        xw = {}
 
-        def widen_part(m, xw, cols):
-            nc.vector.tensor_tensor(out=xw[:, cols], in0=xb[m // 2][:, m % 2, cols].bitcast(FP8), in1=sc[:, cols], op=ALU.mult)
+        def widen_scalar(j, b):
+            if b == 0:
+                t = const.tile([P, 2, D], BF16, name="xw%d" % j)
+                xw[j] = t
+            nc.scalar.copy(out=xw[j][:, b], in_=xb[j][:, b].bitcast(FP8))
 
-        def widen(m):
-            xw = xwp.tile([P, D], BF16, name="xw")
-            widen_part(m, xw, slice(0, D))
-            return xw
+        def widen_vector(j):
+            t = const.tile([P, 2, D], BF16, name="xw%d" % j)
+            xw[j] = t
+            for b in range(2):
+                nc.vector.tensor_copy(out=t[:, b], in_=xb[j][:, b].bitcast(FP8))
 
-        def turn_x(xw, xg, t):
-            words = xw[:].bitcast(F32)
-            keep_warm()
+        def turn_x(j, g):
             tp = pst.tile([P, 2, 2, P], F32, name="tp")
-            for g in range(2):
+            for b in range(2):
+                words = xw[j][:, b].bitcast(F32)
                 for u in range(2):
-                    nc.tensor.transpose(tp[:, g, u, :], words[:, 256 * g + u : 256 * (g + 1) : 2], ident[:])
-            nc.scalar.copy(out=xg[:, t].bitcast(F32), in_=tp[:].rearrange("p g u r -> p g r u"))
+                    nc.tensor.transpose(tp[:, u, b, :], words[:, 256 * g + u : 256 * (g + 1) : 2], ident[:])
+            return tp
 
-        def quant_x(a, xg):
-            nc.vector.quantize_mx(
-                out=xc[a][:].bitcast(FP8X4), scales=xs[a][:], in_=xg[:].rearrange("p t g r k -> p (t g r k)")
+        def scale_vector(g, tp, xg):
+            nc.vector.tensor_tensor(
+                out=xg[:, g].rearrange("p n (u h) -> p n u h", u=2),
+                in0=tp[:].rearrange("p u b r -> p u (b r)").bitcast(BF16).rearrange("p u (n h) -> p n u h", h=2),
+                in1=s8[:, g].rearrange("p (u h) -> p u h", u=2).unsqueeze(1).to_broadcast([P, 2 * P, 2, 2]),
+                op=ALU.mult,
             )
 
-        def turn_w(mat, cc, g, wg, slot=None):
+        def scale_scalar(g, tp, xg):
+            halves = tp[:].rearrange("p u b r -> p u (b r)").bitcast(BF16).rearrange("p u (n h) -> p u n h", h=2)
+            for c in range(4):
+                act(out=xg[:, g, :, c], in_=halves[:, c // 2, :, c % 2], func=ACT.Copy, scale=s8[:, g, c : c + 1])
+
+        def scale_gpsimd(g, tp, xr, xg):
+            nc.scalar.copy(out=xr[:, g].bitcast(F32), in_=tp[:].rearrange("p u b r -> p (b r) u"))
+            nc.gpsimd.tensor_tensor(out=xg[:, g], in0=xr[:, g], in1=s8[:, g].unsqueeze(1).to_broadcast([P, 2 * P, 4]), op=ALU.mult)
+
+        def quant_x(j, xg):
+            nc.vector.quantize_mx(
+                out=xc[j][:].bitcast(FP8X4), scales=xs[j][:], in_=xg[:].rearrange("p g n k -> p (g n k)")
+            )
+
+        wgs = {}
+
+        def turn_w(mat, cc, g):
+            h = cc // 2
+            if cc % 2 == 0:
+                wg = wgp.tile([P, 2, 2, P, 4], BF16, name="wg", align_bytes=64)
+                wgs[(mat, h, g)] = wg
+            wg = wgs[(mat, h, g)]
             words = wr[(mat, cc)][:].bitcast(F32)
-            if mat == 0:
-                keep_warm()
             tp = pst.tile([P, 2, 2, P], F32, name="tp")
             for a in range(2):
                 for u in range(2):
                     nc.tensor.transpose(tp[:, a, u, :], words[:, a, 256 * g + u : 256 * (g + 1) : 2], ident[:])
-            nc.scalar.copy(out=wg[:, cc % 2 if slot is None else slot].bitcast(F32), in_=tp[:].rearrange("p a u r -> p a r u"))
+            if h == 0:
+                nc.scalar.copy(out=wg[:, cc % 2].bitcast(F32), in_=tp[:].rearrange("p a u r -> p a r u"))
+            else:
+                for e in range(2):
+                    nc.scalar.copy(out=wg[:, 1 - e, cc % 2].bitcast(F32), in_=tp[:, e].rearrange("p u r -> p r u"))
 
-        def quant_w(mat, b, g, wg):
-            cols = slice(512 * b, 512 * (b + 1))
-            nc.vector.quantize_mx(
-                out=wc[mat][g][:, cols].bitcast(FP8X4),
-                scales=ws[mat][g][:, cols],
-                in_=wg[:].rearrange("p c a r k -> p (c a r k)"),
+        def quant_w(mat, h):
+            cols = slice(HALF * h, HALF * (h + 1))
+            for g in range(2):
+                nc.vector.quantize_mx(
+                    out=wc[mat][g][:, cols].bitcast(FP8X4),
+                    scales=ws[mat][g][:, cols],
+                    in_=wgs[(mat, h, g)][:].rearrange("p c a r k -> p (c a r k)"),
+                )
+
+        def one_pass(out, j, b, mat, g, cols, start, stop):
+            xcols = slice((2 * g + b) * P, (2 * g + b + 1) * P)
+            nc.tensor.matmul_mx(
+                out=out,
+                lhsT=xc[j][:, xcols].bitcast(FP8X4),
+                lhsT_scale=xs[j][:, xcols],
+                rhs=wc[mat][g][:, cols].bitcast(FP8X4),
+                rhs_scale=ws[mat][g][:, cols],
+                start=start,
+                stop=stop,
             )
 
-        for j in range(2):
-            make_frac(j)
-        first_table = table_calls(0)
-        for call in first_table[4:7]:
-            call()
-        for rep in range(5):
-            nc.tensor.matmul(out=idle_bank[:], lhsT=blank[:, 0:P], rhs=blank[:], start=True, stop=True)
-        for h in range(2):
-            spread_scales(h)
-        for call in first_table[0:4]:
-            call()
-        for j in range(2, 4):
-            make_frac(j)
-        xgs = {}
-        wgs = {}
-        xws = {}
-        for m in range(4):
-            xw_new = xwp.tile([P, D], BF16, name="xw")
-            xws[m] = xw_new
-        for h in range(2):
-            for m in range(2):
-                widen_part(m, xws[m], slice(512 * h, 512 * (h + 1)))
-        for m in range(2, 4):
-            widen_part(m, xws[m], slice(0, D))
-        for a in range(4):
-            xg_new = xgp.tile([P, 2, 2, P, 4], BF16, name="xg", align_bytes=64)
-            xgs[a] = xg_new
-            if a % 2 == 0:
-                for g in range(2):
-                    wg_new = wgp.tile([P, 2, 2, P, 4], BF16, name="wg", align_bytes=64)
-                    wgs[(0, a // 2, g)] = wg_new
-            for g in range(2):
-                turn_w(0, a, g, wgs[(0, a // 2, g)])
-            for t in range(2):
-                turn_x(xws[2 * a + t], xg_new, t)
-            if a < 2:
-                xws[2 * a + 4] = widen(2 * a + 4)
-                xws[2 * a + 5] = widen(2 * a + 5)
-            if a == 2:
-                quant_x(0, xgs[0])
-                quant_x(1, xgs[1])
-        for call in table_calls(1):
-            call()
-        quant_x(2, xgs[2])
-        quant_w(0, 0, 0, wgs[(0, 0, 0)])
-        quant_w(0, 0, 1, wgs[(0, 0, 1)])
-        quant_w(0, 1, 0, wgs[(0, 1, 0)])
-        quant_w(0, 1, 1, wgs[(0, 1, 1)])
-        quant_x(3, xgs[3])
-
-        def products(m, mat, between=None):
-            pr = prp.tile([P, 2, 2, 512], F32, name="pr")
-            tv = tab[m % 4][:].rearrange("p (rep e) i -> p rep i e", rep=2)
+        def passes(step):
+            j, mat, h = step
+            accs = []
             for b in range(2):
-                if b == 1 and between is not None:
-                    between()
-                acc = psa.tile([P, 512], F32, name="acc")
+                acc = psa.tile([P, HALF], F32, name="acc")
+                accs.append(acc)
                 for g in range(2):
-                    xcols = slice((2 * (m % 2) + g) * P, (2 * (m % 2) + g + 1) * P)
-                    nc.tensor.matmul_mx(
-                        out=acc[:],
-                        lhsT=xc[m // 2][:, xcols].bitcast(FP8X4),
-                        lhsT_scale=xs[m // 2][:, xcols],
-                        rhs=wc[mat][g][:, 512 * b : 512 * (b + 1)].bitcast(FP8X4),
-                        rhs_scale=ws[mat][g][:, 512 * b : 512 * (b + 1)],
-                        start=(g == 0),
-                        stop=(g == 1),
+                    one_pass(acc[:], j, b, mat, g, slice(HALF * h, HALF * (h + 1)), g == 0, g == 1)
+            if h == 1:
+                both = pss.tile([P, 2, Q], F32, name="both")
+                accs.append(both)
+                for b in range(2):
+                    for n in range(4):
+                        g, e = n // 2, n % 2
+                        one_pass(both[:, b], j, b, mat, g, slice(HALF + Q * e, HALF + Q * (e + 1)), n == 0, n == 3)
+            return accs
+
+        def products(step, accs):
+            j, mat, h = step
+            pr = prp.tile([P, 4, HALF], F32, name="pr")
+            if h == 0:
+                tv = low[j][:].rearrange("p (rep e) i -> p rep i e", rep=2)
+                for b in range(2):
+                    nc.vector.tensor_tensor(
+                        out=pr[:, 2 * b : 2 * b + 2].rearrange("p rep (i e) -> p rep i e", e=2),
+                        in0=accs[b][:].rearrange("p (i e) -> p i e", e=2).unsqueeze(1).to_broadcast([P, 2, Q, 2]),
+                        in1=tv,
+                        op=ALU.mult,
+                    )
+            else:
+                t = high[j]
+                for b in range(2):
+                    nc.vector.scalar_tensor_tensor(
+                        out=pr[:, b].rearrange("p (i e) -> p i e", e=2),
+                        in0=accs[b][:].rearrange("p (e i) -> p i e", e=2),
+                        scalar=ROOT2,
+                        in1=t[:, 1:3].rearrange("p e i -> p i e"),
+                        op0=ALU.mult,
+                        op1=ALU.mult,
                     )
                 nc.vector.tensor_tensor(
-                    out=pr[:, :, b, :].rearrange("p rep (i e) -> p rep i e", e=2),
-                    in0=acc[:].rearrange("p (i e) -> p i e", e=2).unsqueeze(1).to_broadcast([P, 2, 256, 2]),
-                    in1=tv[:, :, 256 * b : 256 * (b + 1), :],
+                    out=pr[:, 2].rearrange("p (b i) -> p b i", b=2),
+                    in0=accs[2][:],
+                    in1=t[:, 0].unsqueeze(1).to_broadcast([P, 2, Q]),
                     op=ALU.mult,
                 )
             return pr
 
-        def sums(m, mat, pr, on_vector, by_bank=False):
-            ot = otp.tile([P, 2, 256, 2], F32, name="ot")
-            straight = pr[:, 0].rearrange("p b (i e) -> p b i e", e=2)
-            swapped = pr[:, 1].rearrange("p b (i e) -> p b i e", e=2)[:, :, :, ::-1]
-            rows = outs[mat][m * P : (m + 1) * P, :]
-            if on_vector:
-                for b in range(2):
-                    nc.vector.tensor_tensor(out=ot[:, b], in0=straight[:, b], in1=swapped[:, b], op=ALU.add)
-                    nc.sync.dma_start(out=rows[:, 512 * b : 512 * (b + 1)], in_=ot[:, b].rearrange("p i e -> p (i e)"))
-            elif by_bank:
-                for b in range(2):
-                    nc.gpsimd.tensor_tensor(out=ot[:, b], in0=straight[:, b], in1=swapped[:, b], op=ALU.add)
-                nc.sync.dma_start(out=rows, in_=ot[:].rearrange("p b i e -> p (b i e)"))
+        def terms(step, pr):
+            if step[2] == 0:
+                four = pr[:].rearrange("p (b rep) (i e) -> p b rep i e", b=2, e=2)
+                return four[:, :, 0], four[:, :, 1, :, ::-1]
+            common = pr[:, 2].rearrange("p (b i) -> p b i", b=2).unsqueeze(3).to_broadcast([P, 2, Q, 2])
+            return common, pr[:, 0:2].rearrange("p b (i e) -> p b i e", e=2)
+
+        def sums(step, pr, split=False):
+            j, mat, h = step
+            ot = otp.tile([P, 2, Q, 2], F32, name="ot")
+            in0, in1 = terms(step, pr)
+            dst = outs[mat][j][:, :, HALF * h : HALF * (h + 1)]
+            if split:
+                nc.gpsimd.tensor_tensor(out=ot[:, 0], in0=in0[:, 0], in1=in1[:, 0], op=ALU.add)
+                nc.vector.tensor_tensor(out=ot[:, 1], in0=in0[:, 1], in1=in1[:, 1], op=ALU.add)
+                for b in (1, 0):
+                    nc.sync.dma_start(out=dst[:, b], in_=ot[:, b].rearrange("p i e -> p (i e)"))
             else:
-                nc.gpsimd.tensor_tensor(out=ot[:], in0=straight, in1=swapped, op=ALU.add)
-                nc.sync.dma_start(out=rows, in_=ot[:].rearrange("p b i e -> p (b i e)"))
+                nc.gpsimd.tensor_tensor(out=ot[:], in0=in0, in1=in1, op=ALU.add)
+                nc.sync.dma_start(out=dst, in_=ot[:].rearrange("p b i e -> p b (i e)"))
 
-        m_order = [m for j in range(4) for m in (j, j + 4)]
-        k_banks = [(b, g, c) for b in range(2) for g in range(2) for c in range(2)]
-        waiting = []
+        for j in range(4):
+            make_frac(j)
+        warm_bank = pss.tile([P, 2, Q], F32, name="both")
+        for rep in range(6):
+            nc.tensor.matmul(out=warm_bank[:].rearrange("p b i -> p (b i)"), lhsT=blank[:, 0:P], rhs=blank[:], start=True, stop=True)
+        low_table(0)
+        widen_vector(0)
+        xgs = {}
+        banks = {}
 
-        wide = [const.tile([P, 4, 2, P, 4], BF16, name="wide%d" % g, align_bytes=64) for g in range(2)]
+        def new_xg(j):
+            t = xgp.tile([P, 2, 2 * P, 4], BF16, name="xg", align_bytes=64)
+            xgs[j] = t
 
-        def middle_block():
+        def tw(mat, cc):
             for g in range(2):
-                nc.vector.quantize_mx(
-                    out=wc[1][g][:].bitcast(FP8X4), scales=ws[1][g][:], in_=wide[g][:].rearrange("p c a r k -> p (c a r k)")
-                )
+                turn_w(mat, cc, g)
 
-        for idx, m in enumerate(m_order):
-            if idx == 0 or idx == 2:
-                waiting.extend(table_calls(idx // 2 + 2))
-            pr = products(m, 0, middle_block if idx == 7 else None)
-            for b, g, c in k_banks[2 * idx : 2 * idx + 2]:
-                turn_w(1, 2 * b + c, g, wide[g], slot=2 * b + c)
-            for call in waiting[0:4]:
-                call()
-            waiting = waiting[4:]
-            sums(m, 0, pr, False, by_bank=(idx == 6))
-        shared = []
-        for idx, m in enumerate(m_order):
-            pr = products(m, 1)
-            if idx == 6:
-                ot6 = otp.tile([P, 2, 256, 2], F32, name="ot")
-                shared.extend([m, pr, ot6])
-                nc.gpsimd.tensor_tensor(
-                    out=ot6[:, 0],
-                    in0=pr[:, 0, 0].rearrange("p (i e) -> p i e", e=2),
-                    in1=pr[:, 1, 0].rearrange("p (i e) -> p i e", e=2)[:, :, ::-1],
-                    op=ALU.add,
-                )
-            else:
-                if idx == 7:
-                    m6, pr6, ot6 = shared
-                    nc.vector.tensor_tensor(
-                        out=ot6[:, 1],
-                        in0=pr6[:, 0, 1].rearrange("p (i e) -> p i e", e=2),
-                        in1=pr6[:, 1, 1].rearrange("p (i e) -> p i e", e=2)[:, :, ::-1],
-                        op=ALU.add,
-                    )
-                    nc.sync.dma_start(out=outs[1][m6 * P : (m6 + 1) * P, :], in_=ot6[:].rearrange("p b i e -> p (b i e)"))
-                sums(m, 1, pr, idx == 7)
+        def tx(j, g):
+            if g == 0:
+                new_xg(j)
+            banks[(j, g)] = turn_x(j, g)
+
+        def tables(j):
+            low_table(j)
+            high_table(j)
+
+        def xs_scalar(j, g):
+            tx(j, g)
+            scale_scalar(g, banks[(j, g)], xgs[j])
+
+        def xv(j, g):
+            scale_vector(g, banks[(j, g)], xgs[j])
+
+        def new_xr():
+            t = xgp.tile([P, 2, 2 * P, 4], BF16, name="xr", align_bytes=64)
+            banks[-1] = t
+
+        def xg_gpsimd(j, g):
+            scale_gpsimd(g, banks[(j, g)], banks[-1], xgs[j])
+
+        def cast_s(j):
+            widen_scalar(j, 0)
+            widen_scalar(j, 1)
+
+        def qx(j):
+            quant_x(j, xgs[j])
+
+        for g in range(2):
+            tx(0, g)
+            xv(0, g)
+        qx(0)
+        tw(0, 0)
+        tw(0, 1)
+        widen_vector(1)
+        new_xr()
+        for g in range(2):
+            tx(1, g)
+            xg_gpsimd(1, g)
+        quant_w(0, 0)
+        low_table(1)
+
+        order = [(j, mat, h) for mat in range(2) for h in range(2) for j in range(2)] + [(j, mat, h) for j in (2, 3) for mat in range(2) for h in range(2)]
+        plan = {
+            0: (lambda: [], lambda: [tw(0, 2), tw(0, 3), high_table(0), tw(1, 0), high_table(1)], lambda: [quant_w(0, 1), qx(1), go(1)]),
+            1: (lambda: [], lambda: [tw(1, 1)], lambda: []),
+            2: (lambda: [], lambda: [tw(1, 2), cast_s(2)], lambda: [quant_w(1, 0)]),
+            3: (lambda: [], lambda: [tw(1, 3), cast_s(3)], lambda: []),
+            4: (lambda: [], lambda: [xs_scalar(2, 0)], lambda: [quant_w(1, 1)]),
+            5: (lambda: [], lambda: [xs_scalar(2, 1), low_table(2)], lambda: []),
+            6: (lambda: [], lambda: [xs_scalar(3, 0), high_table(2)], lambda: [qx(2)]),
+            7: (lambda: [], lambda: [xs_scalar(3, 1), low_table(3)], lambda: []),
+            8: (lambda: [], lambda: [high_table(3)], lambda: [qx(3)]),
+        }
+        none = (lambda: [], lambda: [], lambda: [])
+        ready = {0: passes(order[0])}
+
+        def go(s):
+            ready[s] = passes(order[s])
+
+        for s in range(16):
+            before, middle, after = plan.get(s, none)
+            before()
+            if s > 0 and s < 15:
+                go(s + 1)
+            middle()
+            pr = products(order[s], ready[s])
+            sums(order[s], pr, split=(s == 15))
+            after()

@@ -21,7 +21,6 @@ HALF = E // 2
 Q = 256
 PI = 3.141592653589793
 RATIO = 10000.0 ** (-1.0 / 512.0)
-ROOT2 = 2.0 ** 0.5
 
 
 def wrap_width(j):
@@ -44,16 +43,14 @@ def tile_ropemaskedattentionhead_pa_kernel(tc, x_bytes, x_scale, w_q, w_k, out_0
         chain = ctx.enter_context(tc.tile_pool(name="chain", bufs=2))
         prp = ctx.enter_context(tc.tile_pool(name="prp", bufs=3))
         otp = ctx.enter_context(tc.tile_pool(name="otp", bufs=4))
-        pst = ctx.enter_context(tc.psum_pool(name="pst", bufs=3))
-        psa = ctx.enter_context(tc.psum_pool(name="psa", bufs=3))
-        pss = ctx.enter_context(tc.psum_pool(name="pss", bufs=2))
+        pst = ctx.enter_context(tc.psum_pool(name="pst", bufs=4))
+        psa = ctx.enter_context(tc.psum_pool(name="psa", bufs=4))
         ctx.enter_context(tc.manual_schedule(engines={mybir.EngineType.DVE, mybir.EngineType.Activation, mybir.EngineType.PE, mybir.EngineType.SP}))
 
         s8 = const.tile([P, 2, 4], F32, name="s8")
         nc.sync.dma_start(out=s8[:], in_=x_scale.rearrange("a b (h p c) -> (a b p) h c", h=2, c=4))
         xview = x_bytes.rearrange("b (j p) k -> j p b k", p=P)
-        straight = [w.rearrange("(cc a p) k -> cc p a k", a=2, p=P) for w in weights]
-        paired = [w.rearrange("(cc p e) k -> cc p e k", e=2, p=P) for w in weights]
+        wviews = [w.rearrange("(cc a p) k -> cc p a k", a=2, p=P) for w in weights]
         xb = {}
         wr = {}
 
@@ -64,7 +61,7 @@ def tile_ropemaskedattentionhead_pa_kernel(tc, x_bytes, x_scale, w_q, w_k, out_0
 
         def load_w(mat, cc):
             t = const.tile([P, 2, D], BF16, name="wr%d%d" % (mat, cc))
-            nc.sync.dma_start(out=t[:], in_=(straight if cc < 2 else paired)[mat][cc])
+            nc.sync.dma_start(out=t[:], in_=wviews[mat][cc])
             wr[(mat, cc)] = t
 
         load_x(0)
@@ -84,14 +81,15 @@ def tile_ropemaskedattentionhead_pa_kernel(tc, x_bytes, x_scale, w_q, w_k, out_0
         make_identity(nc, ident[:])
         ones = const.tile([P, 1], F32, name="ones")
         nc.vector.memset(ones[:], 1.0)
-        blank = const.tile([P, 512], BF16, name="blank")
-        nc.vector.memset(blank[:], 0.0)
         warm = const.tile([P, 1], F32, name="warm")
         nc.scalar.activation(out=warm[:], in_=ones[:], func=ACT.Sin)
         phi = const.tile([P, HALF], F32, name="phi")
+        blank = const.tile([P, 512], BF16, name="blank")
         nc.vector.tensor_scalar(out=phi[:, 0:1], in0=ones[:], scalar1=1.0 / (RATIO * 2.0 * PI), scalar2=None, op0=ALU.mult)
         for s in range(9):
             w = 2 ** s
+            if s < 4:
+                nc.vector.memset(blank[:, 128 * s : 128 * (s + 1)], 0.0)
             nc.vector.tensor_scalar(out=phi[:, w : 2 * w], in0=phi[:, 0:w], scalar1=RATIO ** w, scalar2=None, op0=ALU.mult)
         posp = const.tile([P, 4], F32, name="posp")
         nc.vector.tensor_scalar(out=posp[:], in0=pcol[:], scalar1=2.0 * PI, scalar2=None, op0=ALU.mult)
@@ -109,67 +107,49 @@ def tile_ropemaskedattentionhead_pa_kernel(tc, x_bytes, x_scale, w_q, w_k, out_0
             wc.append([const.tile([P, E], U32, name="wc%d%d" % (mat, g), align_bytes=64) for g in range(2)])
             ws.append([const.tile([P, E], U8, name="ws%d%d" % (mat, g), align_bytes=64) for g in range(2)])
 
+        turns = {}
         fracs = {}
-        low = {}
-        high = {}
+        tables = {}
         act = nc.scalar.activation
+
+        def make_turns(j):
+            n = wrap_width(j)
+            t = chain.tile([P, HALF], I32, name="turns")
+            nc.vector.tensor_scalar(out=t[:, 0:n], in0=phi[:, 0:n], scalar1=pcol[:, j : j + 1], scalar2=None, op0=ALU.mult)
+            turns[j] = t
 
         def make_frac(j):
             n = wrap_width(j)
-            turns = chain.tile([P, HALF], I32, name="turns")
-            nc.vector.tensor_scalar(out=turns[:, 0:n], in0=phi[:, 0:n], scalar1=pcol[:, j : j + 1], scalar2=None, op0=ALU.mult)
-            frac = const.tile([P, HALF], F32, name="frac%d" % j)
+            t = const.tile([P, HALF], F32, name="frac%d" % j)
             nc.vector.scalar_tensor_tensor(
-                out=frac[:, 0:n], in0=phi[:, 0:n], scalar=pcol[:, j : j + 1], in1=turns[:, 0:n], op0=ALU.mult, op1=ALU.subtract
+                out=t[:, 0:n], in0=phi[:, 0:n], scalar=pcol[:, j : j + 1], in1=turns[j][:, 0:n], op0=ALU.mult, op1=ALU.subtract
             )
-            fracs[j] = frac
+            fracs[j] = t
 
-        def low_table(j):
-            n = min(Q, wrap_width(j))
-            frac = fracs[j]
-            t = const.tile([P, 4, Q], F32, name="low%d" % j)
-            low[j] = t
+        def table(j, h):
+            n = min(Q, max(0, wrap_width(j) - Q * h))
+            t = const.tile([P, 4, Q], F32, name="table%d%d" % (j, h))
+            tables[(j, h)] = t
             neg = negp[:, j : j + 1]
             pos = posp[:, j : j + 1]
             if n < Q:
+                rest = phi[:, Q * h + n : Q * (h + 1)]
+                act(out=t[:, 0:2, n:Q], in_=rest.unsqueeze(1).to_broadcast([P, 2, Q - n]), func=ACT.Sin, scale=neg, bias=0.5 * PI)
+                act(out=t[:, 2, n:Q], in_=rest, func=ACT.Sin, scale=neg)
+                act(out=t[:, 3, n:Q], in_=rest, func=ACT.Sin, scale=pos)
+            if n > 0:
+                frac = fracs[j][:, Q * h : Q * h + n]
+                afrac = chain.tile([P, Q], F32, name="afrac")
+                act(out=afrac[:, 0:n], in_=frac, func=ACT.Abs)
+                act(out=t[:, 2, 0:n], in_=frac, func=ACT.Sin, scale=-2.0 * PI)
+                act(out=t[:, 3, 0:n], in_=frac, func=ACT.Sin, scale=2.0 * PI)
                 act(
-                    out=t[:, 0:2, n:Q],
-                    in_=phi[:, n:Q].unsqueeze(1).to_broadcast([P, 2, Q - n]),
+                    out=t[:, 0:2, 0:n],
+                    in_=afrac[:, 0:n].unsqueeze(1).to_broadcast([P, 2, n]),
                     func=ACT.Sin,
-                    scale=neg,
+                    scale=-2.0 * PI,
                     bias=0.5 * PI,
                 )
-                act(out=t[:, 2, n:Q], in_=phi[:, n:Q], func=ACT.Sin, scale=neg)
-                act(out=t[:, 3, n:Q], in_=phi[:, n:Q], func=ACT.Sin, scale=pos)
-            afrac = chain.tile([P, Q], F32, name="afrac")
-            act(out=afrac[:, 0:n], in_=frac[:, 0:n], func=ACT.Abs)
-            act(
-                out=t[:, 0:2, 0:n],
-                in_=afrac[:, 0:n].unsqueeze(1).to_broadcast([P, 2, n]),
-                func=ACT.Sin,
-                scale=-2.0 * PI,
-                bias=0.5 * PI,
-            )
-            act(out=t[:, 2, 0:n], in_=frac[:, 0:n], func=ACT.Sin, scale=-2.0 * PI)
-            act(out=t[:, 3, 0:n], in_=frac[:, 0:n], func=ACT.Sin, scale=2.0 * PI)
-
-        def high_table(j):
-            n = max(Q, wrap_width(j)) - Q
-            t = const.tile([P, 3, Q], F32, name="high%d" % j)
-            high[j] = t
-            neg = negp[:, j : j + 1]
-            pos = posp[:, j : j + 1]
-            rest = phi[:, Q + n : HALF]
-            act(out=t[:, 0, n:Q], in_=rest, func=ACT.Sin, scale=neg, bias=0.5 * PI)
-            act(out=t[:, 1, n:Q], in_=rest, func=ACT.Sin, scale=pos, bias=-0.25 * PI)
-            act(out=t[:, 2, n:Q], in_=rest, func=ACT.Sin, scale=pos, bias=-0.75 * PI)
-            if n > 0:
-                frac = fracs[j][:, Q : Q + n]
-                afrac = chain.tile([P, 3, 32], F32, name="afrac3")
-                for r, shift in enumerate((0.0, 0.125, -0.125)):
-                    act(out=afrac[:, r, 0:n], in_=frac, func=ACT.Abs, bias=shift)
-                act(out=t[:, 0, 0:n], in_=afrac[:, 0, 0:n], func=ACT.Sin, scale=-2.0 * PI, bias=0.5 * PI)
-                act(out=t[:, 1:3, 0:n], in_=afrac[:, 1:3, 0:n], func=ACT.Sin, scale=2.0 * PI, bias=-0.5 * PI)
 
         xw = {}
 
@@ -201,14 +181,16 @@ def tile_ropemaskedattentionhead_pa_kernel(tc, x_bytes, x_scale, w_q, w_k, out_0
                 op=ALU.mult,
             )
 
-        def scale_scalar(g, tp, xg):
-            halves = tp[:].rearrange("p u b r -> p u (b r)").bitcast(BF16).rearrange("p u (n h) -> p u n h", h=2)
-            for c in range(4):
-                act(out=xg[:, g, :, c], in_=halves[:, c // 2, :, c % 2], func=ACT.Copy, scale=s8[:, g, c : c + 1])
-
         def scale_gpsimd(g, tp, xr, xg):
             nc.scalar.copy(out=xr[:, g].bitcast(F32), in_=tp[:].rearrange("p u b r -> p (b r) u"))
             nc.gpsimd.tensor_tensor(out=xg[:, g], in0=xr[:, g], in1=s8[:, g].unsqueeze(1).to_broadcast([P, 2 * P, 4]), op=ALU.mult)
+
+        def scale_scalar(g, tp, xg):
+            halves = tp[:].rearrange("p u b r -> p u (b r)").bitcast(BF16).rearrange("p u (n h) -> p u h n", h=2)
+            planes = xgp.tile([P, 4, 2 * P], BF16, name="xp")
+            for c in range(4):
+                act(out=planes[:, c], in_=halves[:, c // 2, c % 2], func=ACT.Copy, scale=s8[:, g, c : c + 1])
+            nc.scalar.copy(out=xg[:, g], in_=planes[:].rearrange("p c n -> p n c"))
 
         def quant_x(j, xg):
             nc.vector.quantize_mx(
@@ -228,11 +210,7 @@ def tile_ropemaskedattentionhead_pa_kernel(tc, x_bytes, x_scale, w_q, w_k, out_0
             for a in range(2):
                 for u in range(2):
                     nc.tensor.transpose(tp[:, a, u, :], words[:, a, 256 * g + u : 256 * (g + 1) : 2], ident[:])
-            if h == 0:
-                nc.scalar.copy(out=wg[:, cc % 2].bitcast(F32), in_=tp[:].rearrange("p a u r -> p a r u"))
-            else:
-                for e in range(2):
-                    nc.scalar.copy(out=wg[:, 1 - e, cc % 2].bitcast(F32), in_=tp[:, e].rearrange("p u r -> p r u"))
+            nc.scalar.copy(out=wg[:, cc % 2].bitcast(F32), in_=tp[:].rearrange("p a u r -> p a r u"))
 
         def quant_w(mat, h):
             cols = slice(HALF * h, HALF * (h + 1))
@@ -243,94 +221,64 @@ def tile_ropemaskedattentionhead_pa_kernel(tc, x_bytes, x_scale, w_q, w_k, out_0
                     in_=wgs[(mat, h, g)][:].rearrange("p c a r k -> p (c a r k)"),
                 )
 
-        def one_pass(out, j, b, mat, g, cols, start, stop):
-            xcols = slice((2 * g + b) * P, (2 * g + b + 1) * P)
-            nc.tensor.matmul_mx(
-                out=out,
-                lhsT=xc[j][:, xcols].bitcast(FP8X4),
-                lhsT_scale=xs[j][:, xcols],
-                rhs=wc[mat][g][:, cols].bitcast(FP8X4),
-                rhs_scale=ws[mat][g][:, cols],
-                start=start,
-                stop=stop,
-            )
-
         def passes(step):
             j, mat, h = step
+            cols = slice(HALF * h, HALF * (h + 1))
             accs = []
             for b in range(2):
                 acc = psa.tile([P, HALF], F32, name="acc")
                 accs.append(acc)
                 for g in range(2):
-                    one_pass(acc[:], j, b, mat, g, slice(HALF * h, HALF * (h + 1)), g == 0, g == 1)
-            if h == 1:
-                both = pss.tile([P, 2, Q], F32, name="both")
-                accs.append(both)
-                for b in range(2):
-                    for n in range(4):
-                        g, e = n // 2, n % 2
-                        one_pass(both[:, b], j, b, mat, g, slice(HALF + Q * e, HALF + Q * (e + 1)), n == 0, n == 3)
+                    xcols = slice((2 * g + b) * P, (2 * g + b + 1) * P)
+                    nc.tensor.matmul_mx(
+                        out=acc[:],
+                        lhsT=xc[j][:, xcols].bitcast(FP8X4),
+                        lhsT_scale=xs[j][:, xcols],
+                        rhs=wc[mat][g][:, cols].bitcast(FP8X4),
+                        rhs_scale=ws[mat][g][:, cols],
+                        start=(g == 0),
+                        stop=(g == 1),
+                    )
             return accs
 
         def products(step, accs):
             j, mat, h = step
-            pr = prp.tile([P, 4, HALF], F32, name="pr")
-            if h == 0:
-                tv = low[j][:].rearrange("p (rep e) i -> p rep i e", rep=2)
-                for b in range(2):
-                    nc.vector.tensor_tensor(
-                        out=pr[:, 2 * b : 2 * b + 2].rearrange("p rep (i e) -> p rep i e", e=2),
-                        in0=accs[b][:].rearrange("p (i e) -> p i e", e=2).unsqueeze(1).to_broadcast([P, 2, Q, 2]),
-                        in1=tv,
-                        op=ALU.mult,
-                    )
-            else:
-                t = high[j]
-                for b in range(2):
-                    nc.vector.scalar_tensor_tensor(
-                        out=pr[:, b].rearrange("p (i e) -> p i e", e=2),
-                        in0=accs[b][:].rearrange("p (e i) -> p i e", e=2),
-                        scalar=ROOT2,
-                        in1=t[:, 1:3].rearrange("p e i -> p i e"),
-                        op0=ALU.mult,
-                        op1=ALU.mult,
-                    )
+            pr = prp.tile([P, 2, 2, HALF], F32, name="pr")
+            for b in range(2):
                 nc.vector.tensor_tensor(
-                    out=pr[:, 2].rearrange("p (b i) -> p b i", b=2),
-                    in0=accs[2][:],
-                    in1=t[:, 0].unsqueeze(1).to_broadcast([P, 2, Q]),
+                    out=pr[:, b].rearrange("p rep (i e) -> p rep i e", e=2),
+                    in0=accs[b][:].rearrange("p (i e) -> p i e", e=2).unsqueeze(1).to_broadcast([P, 2, Q, 2]),
+                    in1=tables[(j, h)][:].rearrange("p (rep e) i -> p rep i e", rep=2),
                     op=ALU.mult,
                 )
             return pr
 
         def terms(step, pr):
-            if step[2] == 0:
-                four = pr[:].rearrange("p (b rep) (i e) -> p b rep i e", b=2, e=2)
-                return four[:, :, 0], four[:, :, 1, :, ::-1]
-            common = pr[:, 2].rearrange("p (b i) -> p b i", b=2).unsqueeze(3).to_broadcast([P, 2, Q, 2])
-            return common, pr[:, 0:2].rearrange("p b (i e) -> p b i e", e=2)
+            four = pr[:].rearrange("p b rep (i e) -> p b rep i e", e=2)
+            return four[:, :, 0], four[:, :, 1, :, ::-1]
 
-        def sums(step, pr, split=False):
-            j, mat, h = step
-            ot = otp.tile([P, 2, Q, 2], F32, name="ot")
+        def sums(step, pr, engine, ot, batches):
             in0, in1 = terms(step, pr)
-            dst = outs[mat][j][:, :, HALF * h : HALF * (h + 1)]
-            if split:
-                nc.gpsimd.tensor_tensor(out=ot[:, 0], in0=in0[:, 0], in1=in1[:, 0], op=ALU.add)
-                nc.vector.tensor_tensor(out=ot[:, 1], in0=in0[:, 1], in1=in1[:, 1], op=ALU.add)
-                for b in (1, 0):
-                    nc.sync.dma_start(out=dst[:, b], in_=ot[:, b].rearrange("p i e -> p (i e)"))
-            else:
-                nc.gpsimd.tensor_tensor(out=ot[:], in0=in0, in1=in1, op=ALU.add)
-                nc.sync.dma_start(out=dst, in_=ot[:].rearrange("p b i e -> p b (i e)"))
+            for b in batches:
+                engine.tensor_tensor(out=ot[:, b], in0=in0[:, b], in1=in1[:, b], op=ALU.add)
 
-        for j in range(4):
-            make_frac(j)
-        warm_bank = pss.tile([P, 2, Q], F32, name="both")
+        def store(step, ot, b):
+            j, mat, h = step
+            cols = slice(HALF * h, HALF * (h + 1))
+            nc.sync.dma_start(out=outs[mat][j][:, b, cols], in_=ot[:, b].rearrange("p i e -> p (i e)"))
+
+        def finish(step, pr):
+            j, mat, h = step
+            in0, in1 = terms(step, pr)
+            ot = otp.tile([P, 2, Q, 2], F32, name="ot")
+            nc.gpsimd.tensor_tensor(out=ot[:], in0=in0, in1=in1, op=ALU.add)
+            nc.sync.dma_start(out=outs[mat][j][:, :, HALF * h : HALF * (h + 1)], in_=ot[:].rearrange("p b i e -> p b (i e)"))
+
+        make_turns(0)
+        make_frac(0)
+        warm_bank = psa.tile([P, HALF], F32, name="acc")
         for rep in range(6):
-            nc.tensor.matmul(out=warm_bank[:].rearrange("p b i -> p (b i)"), lhsT=blank[:, 0:P], rhs=blank[:], start=True, stop=True)
-        low_table(0)
-        widen_vector(0)
+            nc.tensor.matmul(out=warm_bank[:], lhsT=blank[:, 0:P], rhs=blank[:], start=True, stop=True)
         xgs = {}
         banks = {}
 
@@ -347,16 +295,11 @@ def tile_ropemaskedattentionhead_pa_kernel(tc, x_bytes, x_scale, w_q, w_k, out_0
                 new_xg(j)
             banks[(j, g)] = turn_x(j, g)
 
-        def tables(j):
-            low_table(j)
-            high_table(j)
-
-        def xs_scalar(j, g):
-            tx(j, g)
-            scale_scalar(g, banks[(j, g)], xgs[j])
-
         def xv(j, g):
             scale_vector(g, banks[(j, g)], xgs[j])
+
+        def xs_scalar(j, g):
+            scale_scalar(g, banks[(j, g)], xgs[j])
 
         def new_xr():
             t = xgp.tile([P, 2, 2 * P, 4], BF16, name="xr", align_bytes=64)
@@ -372,6 +315,12 @@ def tile_ropemaskedattentionhead_pa_kernel(tc, x_bytes, x_scale, w_q, w_k, out_0
         def qx(j):
             quant_x(j, xgs[j])
 
+        table(0, 0)
+        widen_vector(0)
+        for j in (1, 2):
+            make_turns(j)
+        for j in (1, 2):
+            make_frac(j)
         for g in range(2):
             tx(0, g)
             xv(0, g)
@@ -384,19 +333,20 @@ def tile_ropemaskedattentionhead_pa_kernel(tc, x_bytes, x_scale, w_q, w_k, out_0
             tx(1, g)
             xg_gpsimd(1, g)
         quant_w(0, 0)
-        low_table(1)
+        table(1, 0)
 
         order = [(j, mat, h) for mat in range(2) for h in range(2) for j in range(2)] + [(j, mat, h) for j in (2, 3) for mat in range(2) for h in range(2)]
         plan = {
-            0: (lambda: [], lambda: [tw(0, 2), tw(0, 3), high_table(0), tw(1, 0), high_table(1)], lambda: [quant_w(0, 1), qx(1), go(1)]),
-            1: (lambda: [], lambda: [tw(1, 1)], lambda: []),
-            2: (lambda: [], lambda: [tw(1, 2), cast_s(2)], lambda: [quant_w(1, 0)]),
-            3: (lambda: [], lambda: [tw(1, 3), cast_s(3)], lambda: []),
-            4: (lambda: [], lambda: [xs_scalar(2, 0)], lambda: [quant_w(1, 1)]),
-            5: (lambda: [], lambda: [xs_scalar(2, 1), low_table(2)], lambda: []),
-            6: (lambda: [], lambda: [xs_scalar(3, 0), high_table(2)], lambda: [qx(2)]),
-            7: (lambda: [], lambda: [xs_scalar(3, 1), low_table(3)], lambda: []),
-            8: (lambda: [], lambda: [high_table(3)], lambda: [qx(3)]),
+            0: (lambda: [], lambda: [tw(0, 2), tw(0, 3), table(0, 1), tw(1, 0), table(1, 1)], lambda: [make_turns(3), make_frac(3), qx(1), go(1), quant_w(0, 1)]),
+            1: (lambda: [], lambda: [tw(1, 1), cast_s(2)], lambda: []),
+            2: (lambda: [], lambda: [tw(1, 2)], lambda: [quant_w(1, 0)]),
+            3: (lambda: [], lambda: [tw(1, 3), tx(2, 0), xs_scalar(2, 0)], lambda: []),
+            4: (lambda: [], lambda: [tx(2, 1), xs_scalar(2, 1)], lambda: [quant_w(1, 1)]),
+            5: (lambda: [], lambda: [table(2, 0), cast_s(3)], lambda: []),
+            6: (lambda: [], lambda: [table(2, 1), tx(3, 0), xs_scalar(3, 0)], lambda: [qx(2)]),
+            7: (lambda: [], lambda: [tx(3, 1), xs_scalar(3, 1), table(3, 0)], lambda: []),
+            8: (lambda: [], lambda: [table(3, 1)], lambda: []),
+            9: (lambda: [], lambda: [], lambda: [qx(3)]),
         }
         none = (lambda: [], lambda: [], lambda: [])
         ready = {0: passes(order[0])}
@@ -404,12 +354,23 @@ def tile_ropemaskedattentionhead_pa_kernel(tc, x_bytes, x_scale, w_q, w_k, out_0
         def go(s):
             ready[s] = passes(order[s])
 
-        for s in range(16):
+        for s in range(14):
             before, middle, after = plan.get(s, none)
             before()
-            if s > 0 and s < 15:
+            if s > 0:
                 go(s + 1)
             middle()
-            pr = products(order[s], ready[s])
-            sums(order[s], pr, split=(s == 15))
+            finish(order[s], products(order[s], ready[s]))
             after()
+        go(15)
+        ot14 = otp.tile([P, 2, Q, 2], F32, name="ot")
+        ot15 = otp.tile([P, 2, Q, 2], F32, name="ot")
+        pr14 = products(order[14], ready[14])
+        sums(order[14], pr14, nc.gpsimd, ot14, (0,))
+        store(order[14], ot14, 0)
+        pr15 = products(order[15], ready[15])
+        sums(order[14], pr14, nc.vector, ot14, (1,))
+        store(order[14], ot14, 1)
+        for b in range(2):
+            sums(order[15], pr15, nc.vector, ot15, (b,))
+            store(order[15], ot15, b)

@@ -21,6 +21,8 @@ HALF = E // 2
 Q = 256
 PI = 3.141592653589793
 RATIO = 10000.0 ** (-1.0 / 512.0)
+ROOT2 = 2.0 ** 0.5
+THREE = ((2, 1), (3, 1))
 
 
 def wrap_width(j):
@@ -40,17 +42,18 @@ def tile_ropemaskedattentionhead_pa_kernel(tc, x_bytes, x_scale, w_q, w_k, out_0
         const = ctx.enter_context(tc.tile_pool(name="const", bufs=1))
         xgp = ctx.enter_context(tc.tile_pool(name="xgp", bufs=3))
         wgp = ctx.enter_context(tc.tile_pool(name="wgp", bufs=6))
-        chain = ctx.enter_context(tc.tile_pool(name="chain", bufs=2))
+        chain = ctx.enter_context(tc.tile_pool(name="chain", bufs=3))
         prp = ctx.enter_context(tc.tile_pool(name="prp", bufs=3))
         otp = ctx.enter_context(tc.tile_pool(name="otp", bufs=4))
-        pst = ctx.enter_context(tc.psum_pool(name="pst", bufs=4))
+        pst = ctx.enter_context(tc.psum_pool(name="pst", bufs=3))
         psa = ctx.enter_context(tc.psum_pool(name="psa", bufs=4))
+        pss = ctx.enter_context(tc.psum_pool(name="pss", bufs=1))
         ctx.enter_context(tc.manual_schedule(engines={mybir.EngineType.DVE, mybir.EngineType.Activation, mybir.EngineType.PE, mybir.EngineType.SP}))
 
         s8 = const.tile([P, 2, 4], F32, name="s8")
         nc.sync.dma_start(out=s8[:], in_=x_scale.rearrange("a b (h p c) -> (a b p) h c", h=2, c=4))
         xview = x_bytes.rearrange("b (j p) k -> j p b k", p=P)
-        wviews = [w.rearrange("(cc a p) k -> cc p a k", a=2, p=P) for w in weights]
+        wviews = [[w.rearrange("(cc a p) k -> cc p a k", a=2, p=P), w.rearrange("(cc p e) k -> cc p e k", e=2, p=P)] for w in weights]
         xb = {}
         wr = {}
 
@@ -61,11 +64,14 @@ def tile_ropemaskedattentionhead_pa_kernel(tc, x_bytes, x_scale, w_q, w_k, out_0
 
         def load_w(mat, cc):
             t = const.tile([P, 2, D], BF16, name="wr%d%d" % (mat, cc))
-            nc.sync.dma_start(out=t[:], in_=wviews[mat][cc])
+            nc.sync.dma_start(out=t[:], in_=wviews[mat][cc // 2][cc])
             wr[(mat, cc)] = t
 
+        first_w = const.tile([P, 2, D], BF16, name="wr00")
+        wr[(0, 0)] = first_w
+        for a in range(2):
+            nc.sync.dma_start(out=first_w[:, a], in_=wviews[0][0][0][:, a])
         load_x(0)
-        load_w(0, 0)
         load_w(0, 1)
         load_x(1)
         load_w(0, 2)
@@ -132,20 +138,31 @@ def tile_ropemaskedattentionhead_pa_kernel(tc, x_bytes, x_scale, w_q, w_k, out_0
             tables[(j, h)] = t
             neg = negp[:, j : j + 1]
             pos = posp[:, j : j + 1]
+            three = (j, h) in THREE
+            c = 2 - h
             if n < Q:
                 rest = phi[:, Q * h + n : Q * (h + 1)]
-                act(out=t[:, 0:2, n:Q], in_=rest.unsqueeze(1).to_broadcast([P, 2, Q - n]), func=ACT.Sin, scale=neg, bias=0.5 * PI)
-                act(out=t[:, 2, n:Q], in_=rest, func=ACT.Sin, scale=neg)
-                act(out=t[:, 3, n:Q], in_=rest, func=ACT.Sin, scale=pos)
+                act(out=t[:, 0:c, n:Q], in_=rest.unsqueeze(1).to_broadcast([P, c, Q - n]), func=ACT.Sin, scale=neg, bias=0.5 * PI)
+                if three:
+                    act(out=t[:, 2, n:Q], in_=rest, func=ACT.Sin, scale=pos, bias=-0.25 * PI)
+                    act(out=t[:, 3, n:Q], in_=rest, func=ACT.Sin, scale=pos, bias=-0.75 * PI)
+                else:
+                    act(out=t[:, 2 + h, n:Q], in_=rest, func=ACT.Sin, scale=neg)
+                    act(out=t[:, 3 - h, n:Q], in_=rest, func=ACT.Sin, scale=pos)
             if n > 0:
                 frac = fracs[j][:, Q * h : Q * h + n]
-                afrac = chain.tile([P, Q], F32, name="afrac")
-                act(out=afrac[:, 0:n], in_=frac, func=ACT.Abs)
-                act(out=t[:, 2, 0:n], in_=frac, func=ACT.Sin, scale=-2.0 * PI)
-                act(out=t[:, 3, 0:n], in_=frac, func=ACT.Sin, scale=2.0 * PI)
+                afrac = chain.tile([P, 3, Q], F32, name="afrac")
+                act(out=afrac[:, 0, 0:n], in_=frac, func=ACT.Abs)
+                if three:
+                    act(out=afrac[:, 1, 0:n], in_=frac, func=ACT.Abs, bias=0.125)
+                    act(out=afrac[:, 2, 0:n], in_=frac, func=ACT.Abs, bias=-0.125)
+                    act(out=t[:, 2:4, 0:n], in_=afrac[:, 1:3, 0:n], func=ACT.Sin, scale=2.0 * PI, bias=-0.5 * PI)
+                else:
+                    act(out=t[:, 2 + h, 0:n], in_=frac, func=ACT.Sin, scale=-2.0 * PI)
+                    act(out=t[:, 3 - h, 0:n], in_=frac, func=ACT.Sin, scale=2.0 * PI)
                 act(
-                    out=t[:, 0:2, 0:n],
-                    in_=afrac[:, 0:n].unsqueeze(1).to_broadcast([P, 2, n]),
+                    out=t[:, 0:c, 0:n],
+                    in_=afrac[:, 0, 0:n].unsqueeze(1).to_broadcast([P, c, n]),
                     func=ACT.Sin,
                     scale=-2.0 * PI,
                     bias=0.5 * PI,
@@ -153,17 +170,15 @@ def tile_ropemaskedattentionhead_pa_kernel(tc, x_bytes, x_scale, w_q, w_k, out_0
 
         xw = {}
 
-        def widen_scalar(j, b):
-            if b == 0:
-                t = const.tile([P, 2, D], BF16, name="xw%d" % j)
-                xw[j] = t
-            nc.scalar.copy(out=xw[j][:, b], in_=xb[j][:, b].bitcast(FP8))
-
-        def widen_vector(j):
+        def new_xw(j):
             t = const.tile([P, 2, D], BF16, name="xw%d" % j)
             xw[j] = t
-            for b in range(2):
-                nc.vector.tensor_copy(out=t[:, b], in_=xb[j][:, b].bitcast(FP8))
+
+        def widen_scalar(j, b):
+            nc.scalar.copy(out=xw[j][:, b], in_=xb[j][:, b].bitcast(FP8))
+
+        def widen_vector(j, b):
+            nc.vector.tensor_copy(out=xw[j][:, b], in_=xb[j][:, b].bitcast(FP8))
 
         def turn_x(j, g):
             tp = pst.tile([P, 2, 2, P], F32, name="tp")
@@ -210,7 +225,11 @@ def tile_ropemaskedattentionhead_pa_kernel(tc, x_bytes, x_scale, w_q, w_k, out_0
             for a in range(2):
                 for u in range(2):
                     nc.tensor.transpose(tp[:, a, u, :], words[:, a, 256 * g + u : 256 * (g + 1) : 2], ident[:])
-            nc.scalar.copy(out=wg[:, cc % 2].bitcast(F32), in_=tp[:].rearrange("p a u r -> p a r u"))
+            if h == 0:
+                nc.scalar.copy(out=wg[:, cc % 2].bitcast(F32), in_=tp[:].rearrange("p a u r -> p a r u"))
+            else:
+                for e in range(2):
+                    nc.scalar.copy(out=wg[:, 1 - e, cc % 2].bitcast(F32), in_=tp[:, e].rearrange("p u r -> p r u"))
 
         def quant_w(mat, h):
             cols = slice(HALF * h, HALF * (h + 1))
@@ -221,41 +240,76 @@ def tile_ropemaskedattentionhead_pa_kernel(tc, x_bytes, x_scale, w_q, w_k, out_0
                     in_=wgs[(mat, h, g)][:].rearrange("p c a r k -> p (c a r k)"),
                 )
 
+        def one_pass(out, j, b, mat, g, cols, start, stop):
+            xcols = slice((2 * g + b) * P, (2 * g + b + 1) * P)
+            nc.tensor.matmul_mx(
+                out=out,
+                lhsT=xc[j][:, xcols].bitcast(FP8X4),
+                lhsT_scale=xs[j][:, xcols],
+                rhs=wc[mat][g][:, cols].bitcast(FP8X4),
+                rhs_scale=ws[mat][g][:, cols],
+                start=start,
+                stop=stop,
+            )
+
         def passes(step):
             j, mat, h = step
-            cols = slice(HALF * h, HALF * (h + 1))
             accs = []
             for b in range(2):
                 acc = psa.tile([P, HALF], F32, name="acc")
                 accs.append(acc)
                 for g in range(2):
-                    xcols = slice((2 * g + b) * P, (2 * g + b + 1) * P)
-                    nc.tensor.matmul_mx(
-                        out=acc[:],
-                        lhsT=xc[j][:, xcols].bitcast(FP8X4),
-                        lhsT_scale=xs[j][:, xcols],
-                        rhs=wc[mat][g][:, cols].bitcast(FP8X4),
-                        rhs_scale=ws[mat][g][:, cols],
-                        start=(g == 0),
-                        stop=(g == 1),
-                    )
+                    one_pass(acc[:], j, b, mat, g, slice(HALF * h, HALF * (h + 1)), g == 0, g == 1)
+            if (j, h) in THREE:
+                both = pss.tile([P, 2, Q], F32, name="both")
+                accs.append(both)
+                for b in range(2):
+                    for n in range(4):
+                        g, e = n // 2, n % 2
+                        one_pass(both[:, b], j, b, mat, g, slice(HALF * h + Q * e, HALF * h + Q * (e + 1)), n == 0, n == 3)
             return accs
 
         def products(step, accs):
             j, mat, h = step
             pr = prp.tile([P, 2, 2, HALF], F32, name="pr")
+            t = tables[(j, h)]
+            if h == 0:
+                for b in range(2):
+                    nc.vector.tensor_tensor(
+                        out=pr[:, b].rearrange("p rep (i e) -> p rep i e", e=2),
+                        in0=accs[b][:].rearrange("p (i e) -> p i e", e=2).unsqueeze(1).to_broadcast([P, 2, Q, 2]),
+                        in1=t[:].rearrange("p (rep e) i -> p rep i e", rep=2),
+                        op=ALU.mult,
+                    )
+                return pr
+            cross = t[:, 2:4].rearrange("p e i -> p i e")
             for b in range(2):
+                odd_even = accs[b][:].rearrange("p (e i) -> p i e", e=2)
+                first = pr[:, b, 0].rearrange("p (i e) -> p i e", e=2)
+                if (j, h) in THREE:
+                    nc.vector.scalar_tensor_tensor(out=first, in0=odd_even, scalar=ROOT2, in1=cross, op0=ALU.mult, op1=ALU.mult)
+                else:
+                    nc.vector.tensor_tensor(out=first, in0=odd_even, in1=cross, op=ALU.mult)
+                    nc.vector.tensor_tensor(
+                        out=pr[:, b, 1].rearrange("p (i e) -> p i e", e=2),
+                        in0=odd_even[:, :, ::-1],
+                        in1=t[:, 0].unsqueeze(2).to_broadcast([P, Q, 2]),
+                        op=ALU.mult,
+                    )
+            if (j, h) in THREE:
                 nc.vector.tensor_tensor(
-                    out=pr[:, b].rearrange("p rep (i e) -> p rep i e", e=2),
-                    in0=accs[b][:].rearrange("p (i e) -> p i e", e=2).unsqueeze(1).to_broadcast([P, 2, Q, 2]),
-                    in1=tables[(j, h)][:].rearrange("p (rep e) i -> p rep i e", rep=2),
-                    op=ALU.mult,
+                    out=pr[:, :, 1, 0:Q], in0=accs[2][:], in1=t[:, 0].unsqueeze(1).to_broadcast([P, 2, Q]), op=ALU.mult
                 )
             return pr
 
         def terms(step, pr):
+            j, mat, h = step
             four = pr[:].rearrange("p b rep (i e) -> p b rep i e", e=2)
-            return four[:, :, 0], four[:, :, 1, :, ::-1]
+            if h == 0:
+                return four[:, :, 0], four[:, :, 1, :, ::-1]
+            if (j, h) in THREE:
+                return four[:, :, 0], pr[:, :, 1, 0:Q].unsqueeze(3).to_broadcast([P, 2, Q, 2])
+            return four[:, :, 0], four[:, :, 1]
 
         def sums(step, pr, engine, ot, batches):
             in0, in1 = terms(step, pr)
@@ -309,6 +363,7 @@ def tile_ropemaskedattentionhead_pa_kernel(tc, x_bytes, x_scale, w_q, w_k, out_0
             scale_gpsimd(g, banks[(j, g)], banks[-1], xgs[j])
 
         def cast_s(j):
+            new_xw(j)
             widen_scalar(j, 0)
             widen_scalar(j, 1)
 
@@ -316,37 +371,43 @@ def tile_ropemaskedattentionhead_pa_kernel(tc, x_bytes, x_scale, w_q, w_k, out_0
             quant_x(j, xgs[j])
 
         table(0, 0)
-        widen_vector(0)
-        for j in (1, 2):
+        for j in (1, 2, 3):
             make_turns(j)
-        for j in (1, 2):
+        for j in (1, 2, 3):
             make_frac(j)
+        new_xw(0)
+        new_xw(1)
+        widen_vector(0, 0)
+        widen_vector(0, 1)
+        tw(0, 0)
+        widen_scalar(1, 0)
+        widen_scalar(1, 1)
         for g in range(2):
             tx(0, g)
+        for g in range(2):
             xv(0, g)
         qx(0)
-        tw(0, 0)
         tw(0, 1)
-        widen_vector(1)
         new_xr()
         for g in range(2):
             tx(1, g)
-            xg_gpsimd(1, g)
+        xg_gpsimd(1, 0)
         quant_w(0, 0)
         table(1, 0)
 
         order = [(j, mat, h) for mat in range(2) for h in range(2) for j in range(2)] + [(j, mat, h) for j in (2, 3) for mat in range(2) for h in range(2)]
         plan = {
-            0: (lambda: [], lambda: [tw(0, 2), tw(0, 3), table(0, 1), tw(1, 0), table(1, 1)], lambda: [make_turns(3), make_frac(3), qx(1), go(1), quant_w(0, 1)]),
+            0: (lambda: [], lambda: [tw(0, 2), tw(0, 3), table(0, 1), tw(1, 0), table(1, 1)], lambda: [xv(1, 1), qx(1), go(1), quant_w(0, 1)]),
             1: (lambda: [], lambda: [tw(1, 1), cast_s(2)], lambda: []),
-            2: (lambda: [], lambda: [tw(1, 2)], lambda: [quant_w(1, 0)]),
-            3: (lambda: [], lambda: [tw(1, 3), tx(2, 0), xs_scalar(2, 0)], lambda: []),
-            4: (lambda: [], lambda: [tx(2, 1), xs_scalar(2, 1)], lambda: [quant_w(1, 1)]),
+            2: (lambda: [], lambda: [tw(1, 2), tx(2, 0), xs_scalar(2, 0)], lambda: [quant_w(1, 0)]),
+            3: (lambda: [], lambda: [tw(1, 3), tx(2, 1), xs_scalar(2, 1)], lambda: []),
+            4: (lambda: [], lambda: [], lambda: [quant_w(1, 1)]),
             5: (lambda: [], lambda: [table(2, 0), cast_s(3)], lambda: []),
             6: (lambda: [], lambda: [table(2, 1), tx(3, 0), xs_scalar(3, 0)], lambda: [qx(2)]),
             7: (lambda: [], lambda: [tx(3, 1), xs_scalar(3, 1), table(3, 0)], lambda: []),
             8: (lambda: [], lambda: [table(3, 1)], lambda: []),
-            9: (lambda: [], lambda: [], lambda: [qx(3)]),
+            9: (lambda: [], lambda: [], lambda: []),
+            10: (lambda: [], lambda: [], lambda: [qx(3)]),
         }
         none = (lambda: [], lambda: [], lambda: [])
         ready = {0: passes(order[0])}
@@ -354,7 +415,7 @@ def tile_ropemaskedattentionhead_pa_kernel(tc, x_bytes, x_scale, w_q, w_k, out_0
         def go(s):
             ready[s] = passes(order[s])
 
-        for s in range(14):
+        for s in range(13):
             before, middle, after = plan.get(s, none)
             before()
             if s > 0:
@@ -362,15 +423,13 @@ def tile_ropemaskedattentionhead_pa_kernel(tc, x_bytes, x_scale, w_q, w_k, out_0
             middle()
             finish(order[s], products(order[s], ready[s]))
             after()
-        go(15)
-        ot14 = otp.tile([P, 2, Q, 2], F32, name="ot")
-        ot15 = otp.tile([P, 2, Q, 2], F32, name="ot")
-        pr14 = products(order[14], ready[14])
-        sums(order[14], pr14, nc.gpsimd, ot14, (0,))
-        store(order[14], ot14, 0)
-        pr15 = products(order[15], ready[15])
-        sums(order[14], pr14, nc.vector, ot14, (1,))
-        store(order[14], ot14, 1)
-        for b in range(2):
-            sums(order[15], pr15, nc.vector, ot15, (b,))
-            store(order[15], ot15, b)
+        last = {}
+        tail_sums = {13: ((13, nc.gpsimd, 0),), 14: ((13, nc.vector, 1), (14, nc.gpsimd, 0),), 15: ((14, nc.vector, 1), (15, nc.gpsimd, 0), (15, nc.vector, 1),)}
+        for s in (13, 14, 15):
+            if s < 15:
+                go(s + 1)
+            ot = otp.tile([P, 2, Q, 2], F32, name="ot")
+            last[s] = (order[s], products(order[s], ready[s]), ot)
+            for step, engine, b in tail_sums[s]:
+                sums(last[step][0], last[step][1], engine, last[step][2], (b,))
+                store(last[step][0], last[step][2], b)

@@ -21,8 +21,6 @@ HALF = E // 2
 Q = 256
 PI = 3.141592653589793
 RATIO = 10000.0 ** (-1.0 / 512.0)
-ROOT2 = 2.0 ** 0.5
-THREE = ((2, 1), (3, 1))
 
 
 def wrap_width(j):
@@ -47,13 +45,13 @@ def tile_ropemaskedattentionhead_pa_kernel(tc, x_bytes, x_scale, w_q, w_k, out_0
         otp = ctx.enter_context(tc.tile_pool(name="otp", bufs=4))
         pst = ctx.enter_context(tc.psum_pool(name="pst", bufs=3))
         psa = ctx.enter_context(tc.psum_pool(name="psa", bufs=4))
-        pss = ctx.enter_context(tc.psum_pool(name="pss", bufs=1))
+        psw = ctx.enter_context(tc.psum_pool(name="psw", bufs=1))
         ctx.enter_context(tc.manual_schedule(engines={mybir.EngineType.DVE, mybir.EngineType.Activation, mybir.EngineType.PE, mybir.EngineType.SP}))
 
         s8 = const.tile([P, 2, 4], F32, name="s8")
         nc.sync.dma_start(out=s8[:], in_=x_scale.rearrange("a b (h p c) -> (a b p) h c", h=2, c=4))
         xview = x_bytes.rearrange("b (j p) k -> j p b k", p=P)
-        wviews = [[w.rearrange("(cc a p) k -> cc p a k", a=2, p=P), w.rearrange("(cc p e) k -> cc p e k", e=2, p=P)] for w in weights]
+        wviews = [w.rearrange("(cc a p) k -> cc p a k", a=2, p=P) for w in weights]
         xb = {}
         wr = {}
 
@@ -64,13 +62,13 @@ def tile_ropemaskedattentionhead_pa_kernel(tc, x_bytes, x_scale, w_q, w_k, out_0
 
         def load_w(mat, cc):
             t = const.tile([P, 2, D], BF16, name="wr%d%d" % (mat, cc))
-            nc.sync.dma_start(out=t[:], in_=wviews[mat][cc // 2][cc])
+            nc.sync.dma_start(out=t[:], in_=wviews[mat][cc])
             wr[(mat, cc)] = t
 
         first_w = const.tile([P, 2, D], BF16, name="wr00")
         wr[(0, 0)] = first_w
         for a in range(2):
-            nc.sync.dma_start(out=first_w[:, a], in_=wviews[0][0][0][:, a])
+            nc.sync.dma_start(out=first_w[:, a], in_=wviews[0][0][:, a])
         load_x(0)
         load_w(0, 1)
         load_x(1)
@@ -138,31 +136,20 @@ def tile_ropemaskedattentionhead_pa_kernel(tc, x_bytes, x_scale, w_q, w_k, out_0
             tables[(j, h)] = t
             neg = negp[:, j : j + 1]
             pos = posp[:, j : j + 1]
-            three = (j, h) in THREE
-            c = 2 - h
             if n < Q:
                 rest = phi[:, Q * h + n : Q * (h + 1)]
-                act(out=t[:, 0:c, n:Q], in_=rest.unsqueeze(1).to_broadcast([P, c, Q - n]), func=ACT.Sin, scale=neg, bias=0.5 * PI)
-                if three:
-                    act(out=t[:, 2, n:Q], in_=rest, func=ACT.Sin, scale=pos, bias=-0.25 * PI)
-                    act(out=t[:, 3, n:Q], in_=rest, func=ACT.Sin, scale=pos, bias=-0.75 * PI)
-                else:
-                    act(out=t[:, 2 + h, n:Q], in_=rest, func=ACT.Sin, scale=neg)
-                    act(out=t[:, 3 - h, n:Q], in_=rest, func=ACT.Sin, scale=pos)
+                act(out=t[:, 0:2, n:Q], in_=rest.unsqueeze(1).to_broadcast([P, 2, Q - n]), func=ACT.Sin, scale=neg, bias=0.5 * PI)
+                act(out=t[:, 2, n:Q], in_=rest, func=ACT.Sin, scale=neg)
+                act(out=t[:, 3, n:Q], in_=rest, func=ACT.Sin, scale=pos)
             if n > 0:
                 frac = fracs[j][:, Q * h : Q * h + n]
-                afrac = chain.tile([P, 3, Q], F32, name="afrac")
-                act(out=afrac[:, 0, 0:n], in_=frac, func=ACT.Abs)
-                if three:
-                    act(out=afrac[:, 1, 0:n], in_=frac, func=ACT.Abs, bias=0.125)
-                    act(out=afrac[:, 2, 0:n], in_=frac, func=ACT.Abs, bias=-0.125)
-                    act(out=t[:, 2:4, 0:n], in_=afrac[:, 1:3, 0:n], func=ACT.Sin, scale=2.0 * PI, bias=-0.5 * PI)
-                else:
-                    act(out=t[:, 2 + h, 0:n], in_=frac, func=ACT.Sin, scale=-2.0 * PI)
-                    act(out=t[:, 3 - h, 0:n], in_=frac, func=ACT.Sin, scale=2.0 * PI)
+                afrac = chain.tile([P, Q], F32, name="afrac")
+                act(out=afrac[:, 0:n], in_=frac, func=ACT.Abs)
+                act(out=t[:, 2, 0:n], in_=frac, func=ACT.Sin, scale=-2.0 * PI)
+                act(out=t[:, 3, 0:n], in_=frac, func=ACT.Sin, scale=2.0 * PI)
                 act(
-                    out=t[:, 0:c, 0:n],
-                    in_=afrac[:, 0, 0:n].unsqueeze(1).to_broadcast([P, c, n]),
+                    out=t[:, 0:2, 0:n],
+                    in_=afrac[:, 0:n].unsqueeze(1).to_broadcast([P, 2, n]),
                     func=ACT.Sin,
                     scale=-2.0 * PI,
                     bias=0.5 * PI,
@@ -225,11 +212,7 @@ def tile_ropemaskedattentionhead_pa_kernel(tc, x_bytes, x_scale, w_q, w_k, out_0
             for a in range(2):
                 for u in range(2):
                     nc.tensor.transpose(tp[:, a, u, :], words[:, a, 256 * g + u : 256 * (g + 1) : 2], ident[:])
-            if h == 0:
-                nc.scalar.copy(out=wg[:, cc % 2].bitcast(F32), in_=tp[:].rearrange("p a u r -> p a r u"))
-            else:
-                for e in range(2):
-                    nc.scalar.copy(out=wg[:, 1 - e, cc % 2].bitcast(F32), in_=tp[:, e].rearrange("p u r -> p r u"))
+            nc.scalar.copy(out=wg[:, cc % 2].bitcast(F32), in_=tp[:].rearrange("p a u r -> p a r u"))
 
         def quant_w(mat, h):
             cols = slice(HALF * h, HALF * (h + 1))
@@ -240,76 +223,41 @@ def tile_ropemaskedattentionhead_pa_kernel(tc, x_bytes, x_scale, w_q, w_k, out_0
                     in_=wgs[(mat, h, g)][:].rearrange("p c a r k -> p (c a r k)"),
                 )
 
-        def one_pass(out, j, b, mat, g, cols, start, stop):
-            xcols = slice((2 * g + b) * P, (2 * g + b + 1) * P)
-            nc.tensor.matmul_mx(
-                out=out,
-                lhsT=xc[j][:, xcols].bitcast(FP8X4),
-                lhsT_scale=xs[j][:, xcols],
-                rhs=wc[mat][g][:, cols].bitcast(FP8X4),
-                rhs_scale=ws[mat][g][:, cols],
-                start=start,
-                stop=stop,
-            )
-
         def passes(step):
             j, mat, h = step
+            cols = slice(HALF * h, HALF * (h + 1))
             accs = []
             for b in range(2):
                 acc = psa.tile([P, HALF], F32, name="acc")
                 accs.append(acc)
                 for g in range(2):
-                    one_pass(acc[:], j, b, mat, g, slice(HALF * h, HALF * (h + 1)), g == 0, g == 1)
-            if (j, h) in THREE:
-                both = pss.tile([P, 2, Q], F32, name="both")
-                accs.append(both)
-                for b in range(2):
-                    for n in range(4):
-                        g, e = n // 2, n % 2
-                        one_pass(both[:, b], j, b, mat, g, slice(HALF * h + Q * e, HALF * h + Q * (e + 1)), n == 0, n == 3)
+                    xcols = slice((2 * g + b) * P, (2 * g + b + 1) * P)
+                    nc.tensor.matmul_mx(
+                        out=acc[:],
+                        lhsT=xc[j][:, xcols].bitcast(FP8X4),
+                        lhsT_scale=xs[j][:, xcols],
+                        rhs=wc[mat][g][:, cols].bitcast(FP8X4),
+                        rhs_scale=ws[mat][g][:, cols],
+                        start=(g == 0),
+                        stop=(g == 1),
+                    )
             return accs
 
         def products(step, accs):
             j, mat, h = step
             pr = prp.tile([P, 2, 2, HALF], F32, name="pr")
-            t = tables[(j, h)]
-            if h == 0:
-                for b in range(2):
-                    nc.vector.tensor_tensor(
-                        out=pr[:, b].rearrange("p rep (i e) -> p rep i e", e=2),
-                        in0=accs[b][:].rearrange("p (i e) -> p i e", e=2).unsqueeze(1).to_broadcast([P, 2, Q, 2]),
-                        in1=t[:].rearrange("p (rep e) i -> p rep i e", rep=2),
-                        op=ALU.mult,
-                    )
-                return pr
-            cross = t[:, 2:4].rearrange("p e i -> p i e")
             for b in range(2):
-                odd_even = accs[b][:].rearrange("p (e i) -> p i e", e=2)
-                first = pr[:, b, 0].rearrange("p (i e) -> p i e", e=2)
-                if (j, h) in THREE:
-                    nc.vector.scalar_tensor_tensor(out=first, in0=odd_even, scalar=ROOT2, in1=cross, op0=ALU.mult, op1=ALU.mult)
-                else:
-                    nc.vector.tensor_tensor(out=first, in0=odd_even, in1=cross, op=ALU.mult)
-                    nc.vector.tensor_tensor(
-                        out=pr[:, b, 1].rearrange("p (i e) -> p i e", e=2),
-                        in0=odd_even[:, :, ::-1],
-                        in1=t[:, 0].unsqueeze(2).to_broadcast([P, Q, 2]),
-                        op=ALU.mult,
-                    )
-            if (j, h) in THREE:
                 nc.vector.tensor_tensor(
-                    out=pr[:, :, 1, 0:Q], in0=accs[2][:], in1=t[:, 0].unsqueeze(1).to_broadcast([P, 2, Q]), op=ALU.mult
+                    out=pr[:, b].rearrange("p rep (i e) -> p rep i e", e=2),
+                    in0=accs[b][:].rearrange("p (i e) -> p i e", e=2).unsqueeze(1).to_broadcast([P, 2, Q, 2]),
+                    in1=tables[(j, h)][:].rearrange("p (rep e) i -> p rep i e", rep=2),
+                    op=ALU.mult,
                 )
             return pr
 
         def terms(step, pr):
-            j, mat, h = step
             four = pr[:].rearrange("p b rep (i e) -> p b rep i e", e=2)
-            if h == 0:
-                return four[:, :, 0], four[:, :, 1, :, ::-1]
-            if (j, h) in THREE:
-                return four[:, :, 0], pr[:, :, 1, 0:Q].unsqueeze(3).to_broadcast([P, 2, Q, 2])
-            return four[:, :, 0], four[:, :, 1]
+            return four[:, :, 0], four[:, :, 1, :, ::-1]
 
         def sums(step, pr, engine, ot, batches):
             in0, in1 = terms(step, pr)
@@ -330,7 +278,7 @@ def tile_ropemaskedattentionhead_pa_kernel(tc, x_bytes, x_scale, w_q, w_k, out_0
 
         make_turns(0)
         make_frac(0)
-        warm_bank = psa.tile([P, HALF], F32, name="acc")
+        warm_bank = psw.tile([P, HALF], F32, name="warm_bank")
         for rep in range(6):
             nc.tensor.matmul(out=warm_bank[:], lhsT=blank[:, 0:P], rhs=blank[:], start=True, stop=True)
         xgs = {}
@@ -415,7 +363,7 @@ def tile_ropemaskedattentionhead_pa_kernel(tc, x_bytes, x_scale, w_q, w_k, out_0
         def go(s):
             ready[s] = passes(order[s])
 
-        for s in range(13):
+        for s in range(14):
             before, middle, after = plan.get(s, none)
             before()
             if s > 0:
@@ -423,13 +371,15 @@ def tile_ropemaskedattentionhead_pa_kernel(tc, x_bytes, x_scale, w_q, w_k, out_0
             middle()
             finish(order[s], products(order[s], ready[s]))
             after()
-        last = {}
-        tail_sums = {13: ((13, nc.gpsimd, 0),), 14: ((13, nc.vector, 1), (14, nc.gpsimd, 0),), 15: ((14, nc.vector, 1), (15, nc.gpsimd, 0), (15, nc.vector, 1),)}
-        for s in (13, 14, 15):
-            if s < 15:
-                go(s + 1)
-            ot = otp.tile([P, 2, Q, 2], F32, name="ot")
-            last[s] = (order[s], products(order[s], ready[s]), ot)
-            for step, engine, b in tail_sums[s]:
-                sums(last[step][0], last[step][1], engine, last[step][2], (b,))
-                store(last[step][0], last[step][2], b)
+        go(15)
+        ot14 = otp.tile([P, 2, Q, 2], F32, name="ot")
+        ot15 = otp.tile([P, 2, Q, 2], F32, name="ot")
+        pr14 = products(order[14], ready[14])
+        sums(order[14], pr14, nc.gpsimd, ot14, (0,))
+        store(order[14], ot14, 0)
+        pr15 = products(order[15], ready[15])
+        sums(order[14], pr14, nc.vector, ot14, (1,))
+        store(order[14], ot14, 1)
+        for b in range(2):
+            sums(order[15], pr15, nc.vector, ot15, (b,))
+            store(order[15], ot15, b)

@@ -155,6 +155,8 @@ def tile_ropemaskedattentionhead_pa_kernel(tc, x_bytes, x_scale, w_q, w_k, out_0
                     bias=0.5 * PI,
                 )
 
+        warm_bank = psw.tile([P, HALF], F32, name="warm_bank")
+
         xw = {}
 
         def new_xw(j):
@@ -167,8 +169,13 @@ def tile_ropemaskedattentionhead_pa_kernel(tc, x_bytes, x_scale, w_q, w_k, out_0
         def widen_vector(j, b):
             nc.vector.tensor_copy(out=xw[j][:, b], in_=xb[j][:, b].bitcast(FP8))
 
+        def keep_warm():
+            nc.tensor.matmul(out=warm_bank[:], lhsT=wr[(0, 0)][:, 0, 0:P], rhs=wr[(0, 0)][:, 0, 0:HALF], start=True, stop=True)
+
         def turn_x(j, g):
             tp = pst.tile([P, 2, 2, P], F32, name="tp")
+            if j == 1:
+                keep_warm()
             for b in range(2):
                 words = xw[j][:, b].bitcast(F32)
                 for u in range(2):
@@ -208,6 +215,8 @@ def tile_ropemaskedattentionhead_pa_kernel(tc, x_bytes, x_scale, w_q, w_k, out_0
                 wgs[(mat, h, g)] = wg
             wg = wgs[(mat, h, g)]
             words = wr[(mat, cc)][:].bitcast(F32)
+            if mat == 0 and cc > 0:
+                keep_warm()
             tp = pst.tile([P, 2, 2, P], F32, name="tp")
             for a in range(2):
                 for u in range(2):
@@ -278,7 +287,6 @@ def tile_ropemaskedattentionhead_pa_kernel(tc, x_bytes, x_scale, w_q, w_k, out_0
 
         make_turns(0)
         make_frac(0)
-        warm_bank = psw.tile([P, HALF], F32, name="warm_bank")
         for rep in range(6):
             nc.tensor.matmul(out=warm_bank[:], lhsT=blank[:, 0:P], rhs=blank[:], start=True, stop=True)
         xgs = {}

@@ -43,8 +43,8 @@ def tile_ropemaskedattentionhead_pa_kernel(tc, x_bytes, x_scale, w_q, w_k, out_0
         chain = ctx.enter_context(tc.tile_pool(name="chain", bufs=3))
         prp = ctx.enter_context(tc.tile_pool(name="prp", bufs=3))
         otp = ctx.enter_context(tc.tile_pool(name="otp", bufs=4))
-        pst = ctx.enter_context(tc.psum_pool(name="pst", bufs=3))
-        psa = ctx.enter_context(tc.psum_pool(name="psa", bufs=4))
+        pst = ctx.enter_context(tc.psum_pool(name="pst", bufs=4))
+        psa = ctx.enter_context(tc.psum_pool(name="psa", bufs=3))
         psw = ctx.enter_context(tc.psum_pool(name="psw", bufs=1))
         ctx.enter_context(tc.manual_schedule(engines={mybir.EngineType.DVE, mybir.EngineType.Activation, mybir.EngineType.PE, mybir.EngineType.SP}))
 
@@ -326,11 +326,12 @@ def tile_ropemaskedattentionhead_pa_kernel(tc, x_bytes, x_scale, w_q, w_k, out_0
         def qx(j):
             quant_x(j, xgs[j])
 
-        table(0, 0)
         for j in (1, 2, 3):
             make_turns(j)
         for j in (1, 2, 3):
             make_frac(j)
+        table(0, 0)
+        table(1, 0)
         new_xw(0)
         new_xw(1)
         widen_vector(0, 0)
@@ -348,12 +349,12 @@ def tile_ropemaskedattentionhead_pa_kernel(tc, x_bytes, x_scale, w_q, w_k, out_0
         for g in range(2):
             tx(1, g)
         xg_gpsimd(1, 0)
+        xs_scalar(1, 1)
         quant_w(0, 0)
-        table(1, 0)
 
         order = [(j, mat, h) for mat in range(2) for h in range(2) for j in range(2)] + [(j, mat, h) for j in (2, 3) for mat in range(2) for h in range(2)]
         plan = {
-            0: (lambda: [], lambda: [tw(0, 2), tw(0, 3), table(0, 1), tw(1, 0), table(1, 1)], lambda: [xv(1, 1), qx(1), go(1), quant_w(0, 1)]),
+            0: (lambda: [], lambda: [tw(0, 2), tw(0, 3), table(0, 1), tw(1, 0), table(1, 1)], lambda: [qx(1), go(1), quant_w(0, 1)]),
             1: (lambda: [], lambda: [tw(1, 1), cast_s(2)], lambda: []),
             2: (lambda: [], lambda: [tw(1, 2), tx(2, 0), xs_scalar(2, 0)], lambda: [quant_w(1, 0)]),
             3: (lambda: [], lambda: [tw(1, 3), tx(2, 1), xs_scalar(2, 1)], lambda: []),

@@ -174,7 +174,7 @@ def tile_ropemaskedattentionhead_pa_kernel(tc, x_bytes, x_scale, w_q, w_k, out_0
 
         def turn_x(j, g):
             tp = pst.tile([P, 2, 2, P], F32, name="tp")
-            if j == 1:
+            if j == 1 and g == 0:
                 keep_warm()
             for b in range(2):
                 words = xw[j][:, b].bitcast(F32)
@@ -215,7 +215,7 @@ def tile_ropemaskedattentionhead_pa_kernel(tc, x_bytes, x_scale, w_q, w_k, out_0
                 wgs[(mat, h, g)] = wg
             wg = wgs[(mat, h, g)]
             words = wr[(mat, cc)][:].bitcast(F32)
-            if mat == 0 and cc > 0:
+            if mat == 0 and cc == 1 and g == 0:
                 keep_warm()
             tp = pst.tile([P, 2, 2, P], F32, name="tp")
             for a in range(2):
@@ -337,10 +337,10 @@ def tile_ropemaskedattentionhead_pa_kernel(tc, x_bytes, x_scale, w_q, w_k, out_0
         widen_vector(0, 0)
         widen_vector(0, 1)
         tw(0, 0)
-        widen_scalar(1, 0)
         widen_scalar(1, 1)
         for g in range(2):
             tx(0, g)
+        widen_vector(1, 0)
         for g in range(2):
             xv(0, g)
         qx(0)

@@ -174,7 +174,7 @@ def tile_ropemaskedattentionhead_pa_kernel(tc, x_bytes, x_scale, w_q, w_k, out_0
 
         def turn_x(j, g):
             tp = pst.tile([P, 2, 2, P], F32, name="tp")
-            if j == 1 and g == 0:
+            if j < 2:
                 keep_warm()
             for b in range(2):
                 words = xw[j][:, b].bitcast(F32)
@@ -215,7 +215,7 @@ def tile_ropemaskedattentionhead_pa_kernel(tc, x_bytes, x_scale, w_q, w_k, out_0
                 wgs[(mat, h, g)] = wg
             wg = wgs[(mat, h, g)]
             words = wr[(mat, cc)][:].bitcast(F32)
-            if mat == 0 and cc == 1 and g == 0:
+            if mat == 0 or cc == 0:
                 keep_warm()
             tp = pst.tile([P, 2, 2, P], F32, name="tp")
             for a in range(2):

from contextlib import ExitStack

import concourse.mybir as mybir
from concourse.masks import make_identity

B, M, D, E = 2, 512, 1024, 1024
FLOPS = 2 * B * M * D * 2 * E

F32 = mybir.dt.float32
BF16 = mybir.dt.bfloat16
U32 = mybir.dt.uint32
I32 = mybir.dt.int32
U8 = mybir.dt.uint8
FP8 = mybir.dt.float8_e4m3fn
FP8X4 = mybir.dt.float8_e4m3fn_x4
ALU = mybir.AluOpType
ACT = mybir.ActivationFunctionType

P = 128
HALF = E // 2
Q = 256
PI = 3.141592653589793
RATIO = 10000.0 ** (-1.0 / 512.0)


def wrap_width(j):
    last = P * (j + 1) - 1
    i = 0
    while last * RATIO ** (i - 1) >= PI:
        i += 1
    return 32 * ((i + 31) // 32)


def tile_ropemaskedattentionhead_pa_kernel(tc, x_bytes, x_scale, w_q, w_k, out_0, out_1):
    nc = tc.nc
    outs = [o.rearrange("b (j p) c -> j p b c", p=P) for o in (out_0, out_1)]
    weights = (w_q, w_k)

    with ExitStack() as ctx:
        const = ctx.enter_context(tc.tile_pool(name="const", bufs=1))
        xgp = ctx.enter_context(tc.tile_pool(name="xgp", bufs=3))
        wgp = ctx.enter_context(tc.tile_pool(name="wgp", bufs=6))
        chain = ctx.enter_context(tc.tile_pool(name="chain", bufs=3))
        prp = ctx.enter_context(tc.tile_pool(name="prp", bufs=3))
        otp = ctx.enter_context(tc.tile_pool(name="otp", bufs=4))
        pst = ctx.enter_context(tc.psum_pool(name="pst", bufs=4))
        psa = ctx.enter_context(tc.psum_pool(name="psa", bufs=3))
        psw = ctx.enter_context(tc.psum_pool(name="psw", bufs=1))
        ctx.enter_context(tc.manual_schedule(engines={mybir.EngineType.DVE, mybir.EngineType.Activation, mybir.EngineType.PE, mybir.EngineType.SP}))

        s8 = const.tile([P, 2, 4], F32, name="s8")
        nc.sync.dma_start(out=s8[:], in_=x_scale.rearrange("a b (h p c) -> (a b p) h c", h=2, c=4))
        xview = x_bytes.rearrange("b (j p) k -> j p b k", p=P)
        wviews = [w.rearrange("(cc a p) k -> cc p a k", a=2, p=P) for w in weights]
        xb = {}
        wr = {}

        def load_x(j):
            t = const.tile([P, 2, D], U8, name="xb%d" % j)
            nc.sync.dma_start(out=t[:], in_=xview[j])
            xb[j] = t

        def load_w(mat, cc):
            t = const.tile([P, 2, D], BF16, name="wr%d%d" % (mat, cc))
            nc.sync.dma_start(out=t[:], in_=wviews[mat][cc])
            wr[(mat, cc)] = t

        first_w = const.tile([P, 2, D], BF16, name="wr00")
        wr[(0, 0)] = first_w
        for a in range(2):
            nc.sync.dma_start(out=first_w[:, a], in_=wviews[0][0][:, a])
        load_x(0)
        load_w(0, 1)
        load_x(1)
        load_w(0, 2)
        load_w(0, 3)
        for cc in range(4):
            load_w(1, cc)
        load_x(2)
        load_x(3)

        pcol = const.tile([P, 4], F32, name="pcol")
        nc.gpsimd.iota(pcol[:], pattern=[[P, 4]], base=0, channel_multiplier=1, allow_small_or_imprecise_dtypes=True)
        ident = const.tile([P, P], F32, name="ident")
        make_identity(nc, ident[:])
        ones = const.tile([P, 1], F32, name="ones")
        nc.vector.memset(ones[:], 1.0)
        warm = const.tile([P, 1], F32, name="warm")
        nc.scalar.activation(out=warm[:], in_=ones[:], func=ACT.Sin)
        phi = const.tile([P, HALF], F32, name="phi")
        blank = const.tile([P, 512], BF16, name="blank")
        nc.vector.tensor_scalar(out=phi[:, 0:1], in0=ones[:], scalar1=1.0 / (RATIO * 2.0 * PI), scalar2=None, op0=ALU.mult)
        for s in range(9):
            w = 2 ** s
            if s < 4:
                nc.vector.memset(blank[:, 128 * s : 128 * (s + 1)], 0.0)
            nc.vector.tensor_scalar(out=phi[:, w : 2 * w], in0=phi[:, 0:w], scalar1=RATIO ** w, scalar2=None, op0=ALU.mult)
        posp = const.tile([P, 4], F32, name="posp")
        nc.vector.tensor_scalar(out=posp[:], in0=pcol[:], scalar1=2.0 * PI, scalar2=None, op0=ALU.mult)
        negp = const.tile([P, 4], F32, name="negp")
        nc.vector.tensor_scalar(out=negp[:], in0=pcol[:], scalar1=-2.0 * PI, scalar2=None, op0=ALU.mult)

        xc = []
        xs = []
        for j in range(4):
            xc.append(const.tile([P, 4 * P], U32, name="xc%d" % j, align_bytes=64))
            xs.append(const.tile([P, 4 * P], U8, name="xs%d" % j, align_bytes=64))
        wc = []
        ws = []
        for mat in range(2):
            wc.append([const.tile([P, E], U32, name="wc%d%d" % (mat, g), align_bytes=64) for g in range(2)])
            ws.append([const.tile([P, E], U8, name="ws%d%d" % (mat, g), align_bytes=64) for g in range(2)])

        turns = {}
        fracs = {}
        tables = {}
        act = nc.scalar.activation

        def make_turns(j):
            n = wrap_width(j)
            t = chain.tile([P, HALF], I32, name="turns")
            nc.vector.tensor_scalar(out=t[:, 0:n], in0=phi[:, 0:n], scalar1=pcol[:, j : j + 1], scalar2=None, op0=ALU.mult)
            turns[j] = t

        def make_frac(j):
            n = wrap_width(j)
            t = const.tile([P, HALF], F32, name="frac%d" % j)
            nc.vector.scalar_tensor_tensor(
                out=t[:, 0:n], in0=phi[:, 0:n], scalar=pcol[:, j : j + 1], in1=turns[j][:, 0:n], op0=ALU.mult, op1=ALU.subtract
            )
            fracs[j] = t

        def table(j, h):
            n = min(Q, max(0, wrap_width(j) - Q * h))
            t = const.tile([P, 4, Q], F32, name="table%d%d" % (j, h))
            tables[(j, h)] = t
            neg = negp[:, j : j + 1]
            pos = posp[:, j : j + 1]
            if n < Q:
                rest = phi[:, Q * h + n : Q * (h + 1)]
                act(out=t[:, 0:2, n:Q], in_=rest.unsqueeze(1).to_broadcast([P, 2, Q - n]), func=ACT.Sin, scale=neg, bias=0.5 * PI)
                act(out=t[:, 2, n:Q], in_=rest, func=ACT.Sin, scale=neg)
                act(out=t[:, 3, n:Q], in_=rest, func=ACT.Sin, scale=pos)
            if n > 0:
                frac = fracs[j][:, Q * h : Q * h + n]
                afrac = chain.tile([P, Q], F32, name="afrac")
                act(out=afrac[:, 0:n], in_=frac, func=ACT.Abs)
                act(out=t[:, 2, 0:n], in_=frac, func=ACT.Sin, scale=-2.0 * PI)
                act(out=t[:, 3, 0:n], in_=frac, func=ACT.Sin, scale=2.0 * PI)
                act(
                    out=t[:, 0:2, 0:n],
                    in_=afrac[:, 0:n].unsqueeze(1).to_broadcast([P, 2, n]),
                    func=ACT.Sin,
                    scale=-2.0 * PI,
                    bias=0.5 * PI,
                )

        warm_bank = psw.tile([P, HALF], F32, name="warm_bank")

        xw = {}

        def new_xw(j):
            t = const.tile([P, 2, D], BF16, name="xw%d" % j)
            xw[j] = t

        def widen_scalar(j, b):
            nc.scalar.copy(out=xw[j][:, b], in_=xb[j][:, b].bitcast(FP8))

        def widen_vector(j, b):
            nc.vector.tensor_copy(out=xw[j][:, b], in_=xb[j][:, b].bitcast(FP8))

        def keep_warm():
            nc.tensor.matmul(out=warm_bank[:], lhsT=wr[(0, 0)][:, 0, 0:P], rhs=wr[(0, 0)][:, 0, 0:HALF], start=True, stop=True)

        def turn_x(j, g):
            tp = pst.tile([P, 2, 2, P], F32, name="tp")
            if j < 2:
                keep_warm()
            for b in range(2):
                words = xw[j][:, b].bitcast(F32)
                for u in range(2):
                    nc.tensor.transpose(tp[:, u, b, :], words[:, 256 * g + u : 256 * (g + 1) : 2], ident[:])
            return tp

        def scale_vector(g, tp, xg):
            nc.vector.tensor_tensor(
                out=xg[:, g].rearrange("p n (u h) -> p n u h", u=2),
                in0=tp[:].rearrange("p u b r -> p u (b r)").bitcast(BF16).rearrange("p u (n h) -> p n u h", h=2),
                in1=s8[:, g].rearrange("p (u h) -> p u h", u=2).unsqueeze(1).to_broadcast([P, 2 * P, 2, 2]),
                op=ALU.mult,
            )

        def scale_gpsimd(g, tp, xr, xg):
            nc.scalar.copy(out=xr[:, g].bitcast(F32), in_=tp[:].rearrange("p u b r -> p (b r) u"))
            nc.gpsimd.tensor_tensor(out=xg[:, g], in0=xr[:, g], in1=s8[:, g].unsqueeze(1).to_broadcast([P, 2 * P, 4]), op=ALU.mult)

        def scale_scalar(g, tp, xg):
            halves = tp[:].rearrange("p u b r -> p u (b r)").bitcast(BF16).rearrange("p u (n h) -> p u h n", h=2)
            planes = xgp.tile([P, 4, 2 * P], BF16, name="xp")
            for c in range(4):
                act(out=planes[:, c], in_=halves[:, c // 2, c % 2], func=ACT.Copy, scale=s8[:, g, c : c + 1])
            nc.scalar.copy(out=xg[:, g], in_=planes[:].rearrange("p c n -> p n c"))

        def quant_x(j, xg):
            nc.vector.quantize_mx(
                out=xc[j][:].bitcast(FP8X4), scales=xs[j][:], in_=xg[:].rearrange("p g n k -> p (g n k)")
            )

        wgs = {}

        def turn_w(mat, cc, g):
            h = cc // 2
            if cc % 2 == 0:
                wg = wgp.tile([P, 2, 2, P, 4], BF16, name="wg", align_bytes=64)
                wgs[(mat, h, g)] = wg
            wg = wgs[(mat, h, g)]
            words = wr[(mat, cc)][:].bitcast(F32)
            if mat == 0 or cc == 0:
                keep_warm()
            tp = pst.tile([P, 2, 2, P], F32, name="tp")
            for a in range(2):
                for u in range(2):
                    nc.tensor.transpose(tp[:, a, u, :], words[:, a, 256 * g + u : 256 * (g + 1) : 2], ident[:])
            nc.scalar.copy(out=wg[:, cc % 2].bitcast(F32), in_=tp[:].rearrange("p a u r -> p a r u"))

        def quant_w(mat, h):
            cols = slice(HALF * h, HALF * (h + 1))
            for g in range(2):
                nc.vector.quantize_mx(
                    out=wc[mat][g][:, cols].bitcast(FP8X4),
                    scales=ws[mat][g][:, cols],
                    in_=wgs[(mat, h, g)][:].rearrange("p c a r k -> p (c a r k)"),
                )

        def passes(step):
            j, mat, h = step
            cols = slice(HALF * h, HALF * (h + 1))
            accs = []
            for b in range(2):
                acc = psa.tile([P, HALF], F32, name="acc")
                accs.append(acc)
                for g in range(2):
                    xcols = slice((2 * g + b) * P, (2 * g + b + 1) * P)
                    nc.tensor.matmul_mx(
                        out=acc[:],
                        lhsT=xc[j][:, xcols].bitcast(FP8X4),
                        lhsT_scale=xs[j][:, xcols],
                        rhs=wc[mat][g][:, cols].bitcast(FP8X4),
                        rhs_scale=ws[mat][g][:, cols],
                        start=(g == 0),
                        stop=(g == 1),
                    )
            return accs

        def products(step, accs):
            j, mat, h = step
            pr = prp.tile([P, 2, 2, HALF], F32, name="pr")
            for b in range(2):
                nc.vector.tensor_tensor(
                    out=pr[:, b].rearrange("p rep (i e) -> p rep i e", e=2),
                    in0=accs[b][:].rearrange("p (i e) -> p i e", e=2).unsqueeze(1).to_broadcast([P, 2, Q, 2]),
                    in1=tables[(j, h)][:].rearrange("p (rep e) i -> p rep i e", rep=2),
                    op=ALU.mult,
                )
            return pr

        def terms(step, pr):
            four = pr[:].rearrange("p b rep (i e) -> p b rep i e", e=2)
            return four[:, :, 0], four[:, :, 1, :, ::-1]

        def sums(step, pr, engine, ot, batches):
            in0, in1 = terms(step, pr)
            for b in batches:
                engine.tensor_tensor(out=ot[:, b], in0=in0[:, b], in1=in1[:, b], op=ALU.add)

        def store(step, ot, b):
            j, mat, h = step
            cols = slice(HALF * h, HALF * (h + 1))
            nc.sync.dma_start(out=outs[mat][j][:, b, cols], in_=ot[:, b].rearrange("p i e -> p (i e)"))

        def finish(step, pr):
            j, mat, h = step
            in0, in1 = terms(step, pr)
            ot = otp.tile([P, 2, Q, 2], F32, name="ot")
            nc.gpsimd.tensor_tensor(out=ot[:], in0=in0, in1=in1, op=ALU.add)
            nc.sync.dma_start(out=outs[mat][j][:, :, HALF * h : HALF * (h + 1)], in_=ot[:].rearrange("p b i e -> p b (i e)"))

        make_turns(0)
        make_frac(0)
        for rep in range(6):
            nc.tensor.matmul(out=warm_bank[:], lhsT=blank[:, 0:P], rhs=blank[:], start=True, stop=True)
        xgs = {}
        banks = {}

        def new_xg(j):
            t = xgp.tile([P, 2, 2 * P, 4], BF16, name="xg", align_bytes=64)
            xgs[j] = t

        def tw(mat, cc):
            for g in range(2):
                turn_w(mat, cc, g)

        def tx(j, g):
            if g == 0:
                new_xg(j)
            banks[(j, g)] = turn_x(j, g)

        def xv(j, g):
            scale_vector(g, banks[(j, g)], xgs[j])

        def xs_scalar(j, g):
            scale_scalar(g, banks[(j, g)], xgs[j])

        def new_xr():
            t = xgp.tile([P, 2, 2 * P, 4], BF16, name="xr", align_bytes=64)
            banks[-1] = t

        def xg_gpsimd(j, g):
            scale_gpsimd(g, banks[(j, g)], banks[-1], xgs[j])

        def cast_s(j):
            new_xw(j)
            widen_scalar(j, 0)
            widen_scalar(j, 1)

        def qx(j):
            quant_x(j, xgs[j])

        for j in (1, 2, 3):
            make_turns(j)
        for j in (1, 2, 3):
            make_frac(j)
        table(0, 0)
        table(1, 0)
        new_xw(0)
        new_xw(1)
        widen_vector(0, 0)
        widen_vector(0, 1)
        tw(0, 0)
        widen_scalar(1, 1)
        for g in range(2):
            tx(0, g)
        widen_vector(1, 0)
        for g in range(2):
            xv(0, g)
        qx(0)
        tw(0, 1)
        new_xr()
        for g in range(2):
            tx(1, g)
        xg_gpsimd(1, 0)
        xs_scalar(1, 1)
        quant_w(0, 0)

        order = [(j, mat, h) for mat in range(2) for h in range(2) for j in range(2)] + [(j, mat, h) for j in (2, 3) for mat in range(2) for h in range(2)]
        plan = {
            0: (lambda: [], lambda: [tw(0, 2), tw(0, 3), table(0, 1), tw(1, 0), table(1, 1)], lambda: [qx(1), go(1), quant_w(0, 1)]),
            1: (lambda: [], lambda: [tw(1, 1), cast_s(2)], lambda: []),
            2: (lambda: [], lambda: [tw(1, 2), tx(2, 0), xs_scalar(2, 0)], lambda: [quant_w(1, 0)]),
            3: (lambda: [], lambda: [tw(1, 3), tx(2, 1), xs_scalar(2, 1)], lambda: []),
            4: (lambda: [], lambda: [], lambda: [quant_w(1, 1)]),
            5: (lambda: [], lambda: [table(2, 0), cast_s(3)], lambda: []),
            6: (lambda: [], lambda: [table(2, 1), tx(3, 0), xs_scalar(3, 0)], lambda: [qx(2)]),
            7: (lambda: [], lambda: [tx(3, 1), xs_scalar(3, 1), table(3, 0)], lambda: []),
            8: (lambda: [], lambda: [table(3, 1)], lambda: []),
            9: (lambda: [], lambda: [], lambda: []),
            10: (lambda: [], lambda: [], lambda: [qx(3)]),
        }
        none = (lambda: [], lambda: [], lambda: [])
        ready = {0: passes(order[0])}

        def go(s):
            ready[s] = passes(order[s])

        for s in range(14):
            before, middle, after = plan.get(s, none)
            before()
            if s > 0:
                go(s + 1)
            middle()
            finish(order[s], products(order[s], ready[s]))
            after()
        go(15)
        ot14 = otp.tile([P, 2, Q, 2], F32, name="ot")
        ot15 = otp.tile([P, 2, Q, 2], F32, name="ot")
        pr14 = products(order[14], ready[14])
        sums(order[14], pr14, nc.gpsimd, ot14, (0,))
        store(order[14], ot14, 0)
        pr15 = products(order[15], ready[15])
        sums(order[14], pr14, nc.vector, ot14, (1,))
        store(order[14], ot14, 1)
        for b in range(2):
            sums(order[15], pr15, nc.vector, ot15, (b,))
            store(order[15], ot15, b)
